import numpy as np
import ml_dtypes


def mxq(x, axis, fmt="e4m3"):
    dtype, down = {"e4m3": (ml_dtypes.float8_e4m3fn, 7), "e5m2": (ml_dtypes.float8_e5m2, 14)}[fmt]
    v = np.moveaxis(np.asarray(x, np.float32).astype(ml_dtypes.bfloat16).astype(np.float64), axis, -1)
    blocks = v.reshape(v.shape[:-1] + (-1, 32))
    amax = np.abs(blocks).max(-1, keepdims=True)
    byte = np.maximum(np.where(amax > 0, np.frexp(amax)[1] - 1 + 127, 0) - down, 1)
    scale = np.exp2(byte - 127.0)
    codes = (blocks / scale).astype(np.float32).astype(dtype).astype(np.float64)
    return np.moveaxis((codes * scale).reshape(v.shape), -1, axis)


WIDE = False


def mx_kscale(k):
    if not WIDE:
        return np.ones(k)
    levels = np.array([10, -10, 5, -5, 0])
    a = np.random.permutation(np.resize(levels, k // 512 * 4)).reshape(k // 512, 4)
    idx = np.arange(k)
    return np.exp2(a[idx // 512, idx % 128 // 32])


BF16 = ml_dtypes.bfloat16


def bf(x):
    return np.asarray(x, np.float32).astype(BF16)


def f64(x):
    return np.asarray(x).astype(np.float64)


B, D, H, O = 8192, 512, 512, 256


def silu(v):
    with np.errstate(over="ignore"):
        return v / (1.0 + np.exp(-v))


def setup_inputs():
    s = mx_kscale(H)
    u = s / s.min()
    return {"t": bf(np.random.random(B)),
            "W1": bf(np.random.standard_normal((H, D)) * 2.0 / np.sqrt(D) * u[:, None]),
            "b1": bf(np.random.standard_normal(H) * 0.5 * u),
            "W2": bf(np.random.standard_normal((O, H)) * 1.5 / np.sqrt(H) / u[None, :]),
            "b2": bf(np.random.standard_normal(O) * 0.5)}


def reference(t, W1, b1, W2, b2):
    t = f64(t)
    phase = (np.arange(D, dtype=np.float64) / D) * np.pi
    tb = t[:, None]
    emb = tb * np.cos(phase[None, :] * tb) + tb * np.sin(phase[None, :] * (1.0 - tb))
    x = silu((mxq(emb, 1, "e4m3") @ mxq(f64(W1), 1, "e4m3").T) + f64(b1))
    x = silu((mxq(x, 1, "e4m3") @ mxq(f64(W2), 1, "e4m3").T) + f64(b2))
    return x

@@ -1,0 +1,221 @@
+import math
+from contextlib import ExitStack
+
+import concourse.mybir as mybir
+from concourse.masks import make_identity
+
+F32 = mybir.dt.float32
+BF16 = mybir.dt.bfloat16
+I32 = mybir.dt.int32
+U32 = mybir.dt.uint32
+U8 = mybir.dt.uint8
+FP8X4 = mybir.dt.float8_e4m3fn_x4
+ACT = mybir.ActivationFunctionType
+ALU = mybir.AluOpType
+
+P = 128
+B, D, H, O = 8192, 512, 512, 256
+FLOPS = 2 * B * D * H + 2 * B * H * O
+
+CB = 1024
+NCH = B // CB
+GB = 512
+NG = B // GB
+LV = 6
+WPREP_AFTER = 1
+
+
+def tile_input_timestep_t_kernel(tc, t, W1, b1, W2, b2, out):
+    nc = tc.nc
+    with ExitStack() as ctx:
+        const = ctx.enter_context(tc.tile_pool(name="const", bufs=1))
+        ring = ctx.enter_context(tc.tile_pool(name="ring", bufs=18))
+        epool = ctx.enter_context(tc.tile_pool(name="epool", bufs=2))
+        gpool = ctx.enter_context(tc.tile_pool(name="gpool", bufs=3))
+        cpool = ctx.enter_context(tc.tile_pool(name="cpool", bufs=6))
+        ypool = ctx.enter_context(tc.tile_pool(name="ypool", bufs=3))
+        psum = ctx.enter_context(tc.psum_pool(name="psum", bufs=4))
+        ctx.enter_context(tc.manual_schedule())
+
+        tb = const.tile([P, B], BF16, name="tb")
+        nc.sync.dma_start(out=tb[:, 0:CB], in_=t[0:CB].partition_broadcast(P))
+        w1raw = ring.tile([P, 4, D], BF16, name="w1raw", tag="ring", align_bytes=64)
+        nc.sync.dma_start(
+            out=w1raw[:].rearrange("p (u e) i -> p u e i", u=2),
+            in_=W1.rearrange("(u p e) i -> p u e i", u=2, e=2),
+        )
+        w2raw = ring.tile([P, 2, H], BF16, name="w2raw", tag="ring", align_bytes=64)
+        nc.sync.dma_start(out=w2raw[:], in_=W2.rearrange("(a p) h -> p a h", a=2))
+        for c in range(1, NCH):
+            nc.sync.dma_start(
+                out=tb[:, c * CB : (c + 1) * CB],
+                in_=t[c * CB : (c + 1) * CB].partition_broadcast(P),
+            )
+        b1raw = const.tile([P, 2, 2], BF16, name="b1raw")
+        b2raw = const.tile([P, 2], BF16, name="b2raw")
+        with nc.allow_non_contiguous_dma(reason="two small bias vectors, one value a partition"):
+            nc.sync.dma_start(out=b1raw[:], in_=b1.rearrange("(u p e) -> p u e", u=2, e=2))
+            nc.sync.dma_start(out=b2raw[:], in_=b2.rearrange("(a p) -> p a", a=2))
+
+        idx_i = const.tile([P, 4], I32, name="idx_i")
+        nc.gpsimd.iota(idx_i[:], pattern=[[256, 2], [1, 2]], base=0, channel_multiplier=2)
+        ident = const.tile([P, P], F32, name="ident")
+        make_identity(nc, ident[:])
+        idx_f = const.tile([P, 4], F32, name="idx_f")
+        nc.vector.tensor_copy(out=idx_f[:], in_=idx_i[:])
+        negphi = const.tile([P, 4], F32, name="negphi")
+        nc.vector.tensor_scalar_mul(out=negphi[:], in0=idx_f[:], scalar1=-math.pi / D)
+        sbias = const.tile([P, 4], F32, name="sbias")
+        nc.vector.tensor_scalar(
+            out=sbias[:], in0=idx_f[:], scalar1=math.pi / (2 * D), scalar2=math.pi / 4,
+            op0=ALU.mult, op1=ALU.add,
+        )
+        csin = const.tile([P, 4], F32, name="csin")
+        nc.scalar.activation(out=csin[:], in_=sbias[:], func=ACT.Sin)
+        amp = const.tile([P, 4], F32, name="amp")
+        nc.vector.tensor_scalar_mul(out=amp[:], in0=csin[:], scalar1=2.0)
+
+        w1c = const.tile([P, H], U32, name="w1c", align_bytes=64)
+        w1s = const.tile([P, H], U8, name="w1s", align_bytes=64)
+        w2c = const.tile([P, O], U32, name="w2c", align_bytes=64)
+        w2s = const.tile([P, O], U8, name="w2s", align_bytes=64)
+        b1f = const.tile([P, 4], F32, name="b1f")
+        b2f = const.tile([P, 2], F32, name="b2f")
+        wts = []
+        for a in range(3):
+            wt = psum.tile([P, 2, 2, P], F32, name="wt", tag="mm")
+            for m in range(2):
+                src = w1raw[:, 2 * a + m, :] if a < 2 else w2raw[:, m, :]
+                for u in range(2):
+                    nc.tensor.transpose(
+                        wt[:, m, u, :], src.bitcast(F32)[:, u * P : (u + 1) * P], ident[:]
+                    )
+            wts.append(wt)
+
+        def weight_prep():
+            w1g = ring.tile([P, 4, P, 4], BF16, name="w1g", tag="ring", align_bytes=64)
+            w2g = ring.tile([P, 2, P, 4], BF16, name="w2g", tag="ring", align_bytes=64)
+            w1gw = w1g[:].bitcast(F32)
+            for a in range(2):
+                nc.vector.tensor_copy(
+                    out=w1gw[:, 2 * a : 2 * a + 2, :, :],
+                    in_=wts[a][:].rearrange("p m u h -> p m h u"),
+                )
+            nc.vector.tensor_copy(
+                out=w2g[:].bitcast(F32), in_=wts[2][:].rearrange("p m u h -> p m h u")
+            )
+            nc.vector.quantize_mx(
+                out=w1c[:].bitcast(FP8X4), scales=w1s[:],
+                in_=w1g[:].rearrange("p m h k -> p (m h k)"),
+            )
+            nc.vector.quantize_mx(
+                out=w2c[:].bitcast(FP8X4), scales=w2s[:],
+                in_=w2g[:].rearrange("p m h k -> p (m h k)"),
+            )
+            nc.vector.tensor_copy(out=b1f[:], in_=b1raw[:].rearrange("p u e -> p (u e)"))
+            nc.vector.tensor_copy(out=b2f[:], in_=b2raw[:])
+
+        def regroup(dst, src):
+            nc.vector.tensor_copy(
+                out=dst.rearrange("p (c i k) -> p c k i", i=4, k=4),
+                in_=src.rearrange("p k (c i) -> p c k i", i=4),
+            )
+
+        ec = const.tile([P, B], U32, name="ec", align_bytes=64)
+        es = const.tile([P, B], U8, name="es", align_bytes=64)
+        for c in range(NCH):
+            cols = slice(c * CB, (c + 1) * CB)
+            ep = epool.tile([P, 4, CB], BF16, name="ep")
+            for m in range(4):
+                sn = ring.tile([P, CB], F32, name="sn", tag="ring", align_bytes=64)
+                nc.scalar.activation(
+                    out=sn[:], in_=tb[:, cols], func=ACT.Sin,
+                    bias=sbias[:, m : m + 1], scale=negphi[:, m : m + 1],
+                )
+                nc.vector.scalar_tensor_tensor(
+                    out=ep[:, m, :], in0=sn[:], scalar=amp[:, m : m + 1], in1=tb[:, cols],
+                    op0=ALU.mult, op1=ALU.mult,
+                )
+            egs = []
+            for s in range(2):
+                eg = gpool.tile([P, 4 * GB], BF16, name="eg", tag="grouped", align_bytes=64)
+                regroup(eg[:], ep[:, :, s * GB : (s + 1) * GB])
+                egs.append(eg)
+            for s in range(2):
+                half = slice(c * CB + s * GB, c * CB + (s + 1) * GB)
+                nc.vector.quantize_mx(
+                    out=ec[:, half].bitcast(FP8X4), scales=es[:, half], in_=egs[s][:]
+                )
+            if c == WPREP_AFTER:
+                weight_prep()
+
+        hps = []
+        for g in range(NG):
+            cols = slice(g * GB, (g + 1) * GB)
+            hp = ring.tile([P, 4, GB], BF16, name="hp", tag="ring", align_bytes=64)
+            hps.append(hp)
+            for m in range(4):
+                ps1 = psum.tile([P, GB], F32, name="ps1", tag="mm")
+                nc.tensor.matmul_mx(
+                    out=ps1[:],
+                    lhsT=w1c[:, m * P : (m + 1) * P].bitcast(FP8X4),
+                    lhsT_scale=w1s[:, m * P : (m + 1) * P],
+                    rhs=ec[:, cols].bitcast(FP8X4),
+                    rhs_scale=es[:, cols],
+                    start=True, stop=True,
+                )
+                nc.scalar.activation(
+                    out=hp[:, m, :], in_=ps1[:], func=ACT.Silu, bias=b1f[:, m : m + 1], scale=1.0
+                )
+
+        out_v = out.rearrange("(g a p) o -> g p a o", a=4, p=P)
+        hgs, yts, ps3s, yos = {}, {}, {}, {}
+        for k in range(NG + LV + 1):
+            if k < NG:
+                hgs[k] = gpool.tile([P, 4 * GB], BF16, name="hg", tag="grouped", align_bytes=64)
+                regroup(hgs[k][:], hps[k][:])
+            g = k - 1
+            if 0 <= g < NG:
+                hc = cpool.tile([P, GB], U32, name="hc", align_bytes=64)
+                hs = cpool.tile([P, GB], U8, name="hs", align_bytes=64)
+                nc.vector.quantize_mx(out=hc[:].bitcast(FP8X4), scales=hs[:], in_=hgs[g][:])
+            gv = k - LV
+            if 0 <= gv < NG:
+                nc.vector.tensor_copy(out=yos[gv][:, 0:2, :], in_=ps3s[gv, 0][:])
+                nc.sync.dma_start(out=out_v[gv], in_=yos[gv][:])
+            if 0 <= g < NG:
+                ps2s = []
+                for a in range(2):
+                    ps2 = psum.tile([P, GB], F32, name="ps2", tag="mm")
+                    nc.tensor.matmul_mx(
+                        out=ps2[:],
+                        lhsT=w2c[:, a * P : (a + 1) * P].bitcast(FP8X4),
+                        lhsT_scale=w2s[:, a * P : (a + 1) * P],
+                        rhs=hc[:].bitcast(FP8X4),
+                        rhs_scale=hs[:],
+                        start=True, stop=True,
+                    )
+                    ps2s.append(ps2)
+            gt = k - 2
+            if 0 <= gt < NG:
+                for half in range(2):
+                    ps3 = psum.tile([P, 2, O], F32, name="ps3", tag="tr")
+                    ps3s[gt, half] = ps3
+                    for j in range(2):
+                        bt = 2 * half + j
+                        for a in range(2):
+                            nc.tensor.transpose(
+                                ps3[:, j, a * P : (a + 1) * P],
+                                yts[gt][:, a, bt * P : (bt + 1) * P],
+                                ident[:],
+                            )
+            if 0 <= g < NG:
+                yts[g] = ypool.tile([P, 2, GB], F32, name="yt")
+                for a in range(2):
+                    nc.scalar.activation(
+                        out=yts[g][:, a, :], in_=ps2s[a][:], func=ACT.Silu,
+                        bias=b2f[:, a : a + 1], scale=1.0,
+                    )
+            if 0 <= gt < NG:
+                yos[gt] = ypool.tile([P, 4, O], F32, name="yo", bufs=5)
+                nc.scalar.copy(out=yos[gt][:, 2:4, :], in_=ps3s[gt, 1][:])

@@ -17,40 +17,64 @@ P = 128
 B, D, H, O = 8192, 512, 512, 256
 FLOPS = 2 * B * D * H + 2 * B * H * O
 
-CB = 1024
-NCH = B // CB
 GB = 512
 NG = B // GB
-LV = 6
-WPREP_AFTER = 1
+FIRST = 256
+TLOAD = 1024
+TC_GROUPS = tuple(range(1, 10))
+N_AHEAD = 12
+K = 4
+N_SCALAR_COPIES = 6
+WPREP_AFTER = 3
+
+
+def fill_count(k):
+    if k < K:
+        return 1
+    return 3 if k == K else 2
+
+
+def copied_by_scalar(g, half):
+    return half == 1 and (g < N_SCALAR_COPIES or g == NG - 1)
 
 
 def tile_input_timestep_t_kernel(tc, t, W1, b1, W2, b2, out):
     nc = tc.nc
     with ExitStack() as ctx:
         const = ctx.enter_context(tc.tile_pool(name="const", bufs=1))
-        ring = ctx.enter_context(tc.tile_pool(name="ring", bufs=18))
+        snpool = ctx.enter_context(tc.tile_pool(name="snpool", bufs=8))
         epool = ctx.enter_context(tc.tile_pool(name="epool", bufs=2))
-        gpool = ctx.enter_context(tc.tile_pool(name="gpool", bufs=3))
-        cpool = ctx.enter_context(tc.tile_pool(name="cpool", bufs=6))
+        gpool = ctx.enter_context(tc.tile_pool(name="gpool", bufs=4))
+        hpool = ctx.enter_context(tc.tile_pool(name="hpool", bufs=7))
+        cpool = ctx.enter_context(tc.tile_pool(name="cpool", bufs=4))
         ypool = ctx.enter_context(tc.tile_pool(name="ypool", bufs=3))
-        psum = ctx.enter_context(tc.psum_pool(name="psum", bufs=4))
+        psum = ctx.enter_context(tc.psum_pool(name="psum", bufs=1))
         ctx.enter_context(tc.manual_schedule())
 
+        def mm_bank(shape, dtype, name):
+            return psum.tile(shape, dtype, name=name, tag="mm", bufs=5)
+
+        def tr_bank(shape, dtype, name):
+            return psum.tile(shape, dtype, name=name, tag="tr", bufs=3)
+
         tb = const.tile([P, B], BF16, name="tb")
-        nc.sync.dma_start(out=tb[:, 0:CB], in_=t[0:CB].partition_broadcast(P))
-        w1raw = ring.tile([P, 4, D], BF16, name="w1raw", tag="ring", align_bytes=64)
+        cuts = [0, FIRST] + list(range(TLOAD, B + 1, TLOAD))
+
+        def load_t(i):
+            lo, hi = cuts[i], cuts[i + 1]
+            nc.sync.dma_start(out=tb[:, lo:hi], in_=t[lo:hi].partition_broadcast(P))
+
+        for i in range(3):
+            load_t(i)
+        w1raw = hpool.tile([P, 4, D], BF16, name="w1raw", tag="hp", align_bytes=64)
         nc.sync.dma_start(
             out=w1raw[:].rearrange("p (u e) i -> p u e i", u=2),
             in_=W1.rearrange("(u p e) i -> p u e i", u=2, e=2),
         )
-        w2raw = ring.tile([P, 2, H], BF16, name="w2raw", tag="ring", align_bytes=64)
+        w2raw = hpool.tile([P, 2, H], BF16, name="w2raw", tag="hp", align_bytes=64)
         nc.sync.dma_start(out=w2raw[:], in_=W2.rearrange("(a p) h -> p a h", a=2))
-        for c in range(1, NCH):
-            nc.sync.dma_start(
-                out=tb[:, c * CB : (c + 1) * CB],
-                in_=t[c * CB : (c + 1) * CB].partition_broadcast(P),
-            )
+        for i in range(3, len(cuts) - 1):
+            load_t(i)
         b1raw = const.tile([P, 2, 2], BF16, name="b1raw")
         b2raw = const.tile([P, 2], BF16, name="b2raw")
         with nc.allow_non_contiguous_dma(reason="two small bias vectors, one value a partition"):
@@ -59,6 +83,10 @@ def tile_input_timestep_t_kernel(tc, t, W1, b1, W2, b2, out):
 
         idx_i = const.tile([P, 4], I32, name="idx_i")
         nc.gpsimd.iota(idx_i[:], pattern=[[256, 2], [1, 2]], base=0, channel_multiplier=2)
+        xt = const.tile([P, 4, P], BF16, name="xt")
+        nc.gpsimd.memset(xt[:], 0.0)
+        identb = const.tile([P, P], BF16, name="identb")
+        make_identity(nc, identb[:])
         ident = const.tile([P, P], F32, name="ident")
         make_identity(nc, ident[:])
         idx_f = const.tile([P, 4], F32, name="idx_f")
@@ -74,6 +102,18 @@ def tile_input_timestep_t_kernel(tc, t, W1, b1, W2, b2, out):
         nc.scalar.activation(out=csin[:], in_=sbias[:], func=ACT.Sin)
         amp = const.tile([P, 4], F32, name="amp")
         nc.vector.tensor_scalar_mul(out=amp[:], in0=csin[:], scalar1=2.0)
+        rest1 = const.tile([P, 4], F32, name="rest1")
+        rest2 = const.tile([P, 4], F32, name="rest2")
+        nc.vector.tensor_copy(out=xt[:, :, 0], in_=amp[:])
+        nc.vector.tensor_tensor(out=rest1[:], in0=amp[:], in1=xt[:, :, 0], op=ALU.subtract)
+        nc.vector.tensor_copy(out=xt[:, :, 1], in_=rest1[:])
+        nc.vector.tensor_tensor(out=rest2[:], in0=rest1[:], in1=xt[:, :, 1], op=ALU.subtract)
+        nc.vector.tensor_copy(out=xt[:, :, 2], in_=rest2[:])
+        clp = tr_bank([P, 4, P], BF16, "clp")
+        for j in range(4):
+            nc.tensor.transpose(clp[:, j, :], xt[:, j, :], identb[:])
+        cl = const.tile([P, 4, P], BF16, name="cl")
+        nc.vector.tensor_copy(out=cl[:], in_=clp[:])
 
         w1c = const.tile([P, H], U32, name="w1c", align_bytes=64)
         w1s = const.tile([P, H], U8, name="w1s", align_bytes=64)
@@ -83,7 +123,7 @@ def tile_input_timestep_t_kernel(tc, t, W1, b1, W2, b2, out):
         b2f = const.tile([P, 2], F32, name="b2f")
         wts = []
         for a in range(3):
-            wt = psum.tile([P, 2, 2, P], F32, name="wt", tag="mm")
+            wt = mm_bank([P, 2, 2, P], F32, "wt")
             for m in range(2):
                 src = w1raw[:, 2 * a + m, :] if a < 2 else w2raw[:, m, :]
                 for u in range(2):
@@ -93,8 +133,8 @@ def tile_input_timestep_t_kernel(tc, t, W1, b1, W2, b2, out):
             wts.append(wt)
 
         def weight_prep():
-            w1g = ring.tile([P, 4, P, 4], BF16, name="w1g", tag="ring", align_bytes=64)
-            w2g = ring.tile([P, 2, P, 4], BF16, name="w2g", tag="ring", align_bytes=64)
+            w1g = hpool.tile([P, 4, P, 4], BF16, name="w1g", tag="hp", align_bytes=64)
+            w2g = hpool.tile([P, 2, P, 4], BF16, name="w2g", tag="hp", align_bytes=64)
             w1gw = w1g[:].bitcast(F32)
             for a in range(2):
                 nc.vector.tensor_copy(
@@ -123,99 +163,193 @@ def tile_input_timestep_t_kernel(tc, t, W1, b1, W2, b2, out):
 
         ec = const.tile([P, B], U32, name="ec", align_bytes=64)
         es = const.tile([P, B], U8, name="es", align_bytes=64)
-        for c in range(NCH):
-            cols = slice(c * CB, (c + 1) * CB)
-            ep = epool.tile([P, 4, CB], BF16, name="ep")
-            for m in range(4):
-                sn = ring.tile([P, CB], F32, name="sn", tag="ring", align_bytes=64)
-                nc.scalar.activation(
-                    out=sn[:], in_=tb[:, cols], func=ACT.Sin,
-                    bias=sbias[:, m : m + 1], scale=negphi[:, m : m + 1],
-                )
-                nc.vector.scalar_tensor_tensor(
-                    out=ep[:, m, :], in0=sn[:], scalar=amp[:, m : m + 1], in1=tb[:, cols],
-                    op0=ALU.mult, op1=ALU.mult,
-                )
-            egs = []
-            for s in range(2):
-                eg = gpool.tile([P, 4 * GB], BF16, name="eg", tag="grouped", align_bytes=64)
-                regroup(eg[:], ep[:, :, s * GB : (s + 1) * GB])
-                egs.append(eg)
-            for s in range(2):
-                half = slice(c * CB + s * GB, c * CB + (s + 1) * GB)
-                nc.vector.quantize_mx(
-                    out=ec[:, half].bitcast(FP8X4), scales=es[:, half], in_=egs[s][:]
-                )
-            if c == WPREP_AFTER:
-                weight_prep()
+        sns, eps, egs = {}, {}, {}
 
-        hps = []
-        for g in range(NG):
+        def pieces_of(g):
+            return [(0, FIRST), (FIRST, GB)] if g == 0 else [(0, GB)]
+
+        def sines(g):
+            sns[g] = snpool.tile([P, 4, GB], F32, name="sn")
+            for lo, hi in pieces_of(g):
+                for m in range(4):
+                    nc.scalar.activation(
+                        out=sns[g][:, m, lo:hi], in_=tb[:, g * GB + lo : g * GB + hi], func=ACT.Sin,
+                        bias=sbias[:, m : m + 1], scale=negphi[:, m : m + 1],
+                    )
+
+        def grouped_tile(g):
+            egs[g] = gpool.tile([P, 4 * GB], BF16, name="eg", tag="grouped", align_bytes=64)
+
+        def amplitude_plane(g, lo, hi, m):
+            if g not in eps:
+                eps[g] = epool.tile([P, 4, GB], BF16, name="ep")
+            nc.vector.scalar_tensor_tensor(
+                out=eps[g][:, m, lo:hi], in0=sns[g][:, m, lo:hi], scalar=amp[:, m : m + 1],
+                in1=tb[:, g * GB + lo : g * GB + hi], op0=ALU.mult, op1=ALU.mult,
+            )
+
+        def regroup_embedding(g):
+            grouped_tile(g)
+            regroup(egs[g][:], eps[g][:])
+
+        def amplitude_grouped(g, q):
+            if q == 0:
+                grouped_tile(g)
+            bank = tr_bank([P, 4, P], F32, "tcb")
+            cols = slice(g * GB + q * P, g * GB + (q + 1) * P)
+            for j in range(4):
+                nc.tensor.matmul(
+                    out=bank[:, j, :], lhsT=cl[:, j, :], rhs=tb[:, cols], start=True, stop=True
+                )
+            nc.vector.tensor_tensor(
+                out=egs[g][:, q * 4 * P : (q + 1) * 4 * P].rearrange("p (b j) -> p b j", j=4),
+                in0=bank[:].rearrange("p j b -> p b j"),
+                in1=sns[g][:, :, q * P : (q + 1) * P].rearrange("p j b -> p b j"),
+                op=ALU.mult,
+            )
+
+        def quantise_embedding(g):
             cols = slice(g * GB, (g + 1) * GB)
-            hp = ring.tile([P, 4, GB], BF16, name="hp", tag="ring", align_bytes=64)
-            hps.append(hp)
+            nc.vector.quantize_mx(out=ec[:, cols].bitcast(FP8X4), scales=es[:, cols], in_=egs[g][:])
+
+        stream = []
+        for g in range(NG):
+            if g in TC_GROUPS:
+                work = [(g, amplitude_grouped, (g, q)) for q in range(4)]
+            else:
+                work = [
+                    (g, amplitude_plane, (g, lo, hi, m)) for lo, hi in pieces_of(g) for m in range(4)
+                ] + [(g, regroup_embedding, (g,))]
+            stream.append(work[0])
+            if g > 0:
+                stream.append((g, quantise_embedding, (g - 1,)))
+            stream.extend(work[1:])
+            if g == WPREP_AFTER:
+                stream.append((g, weight_prep, ()))
+        stream.append((NG - 1, quantise_embedding, (NG - 1,)))
+        position = [0]
+
+        def embedding_step():
+            if position[0] < len(stream):
+                g, call, args = stream[position[0]]
+                position[0] += 1
+                if g not in sns:
+                    sines(g)
+                call(*args)
+
+        ahead = stream.index((N_AHEAD, quantise_embedding, (N_AHEAD - 1,))) + 1
+        for i in range(ahead):
+            embedding_step()
+        for g in range(NG):
+            if g not in sns:
+                sines(g)
+
+        out_v = out.rearrange("(g s a p) o -> g s p a o", s=2, a=2, p=P)
+        ps1s, hps, hgs, hcs, ps2s, yts, ps3s = {}, {}, {}, {}, {}, {}, {}
+
+        def layer1(g):
+            cols = slice(g * GB, (g + 1) * GB)
             for m in range(4):
-                ps1 = psum.tile([P, GB], F32, name="ps1", tag="mm")
+                ps1s[g, m] = mm_bank([P, GB], F32, "ps1")
                 nc.tensor.matmul_mx(
-                    out=ps1[:],
+                    out=ps1s[g, m][:],
                     lhsT=w1c[:, m * P : (m + 1) * P].bitcast(FP8X4),
                     lhsT_scale=w1s[:, m * P : (m + 1) * P],
                     rhs=ec[:, cols].bitcast(FP8X4),
                     rhs_scale=es[:, cols],
                     start=True, stop=True,
                 )
+
+        def silu1(g):
+            hps[g] = hpool.tile([P, 4, GB], BF16, name="hp", tag="hp", align_bytes=64)
+            for m in range(4):
                 nc.scalar.activation(
-                    out=hp[:, m, :], in_=ps1[:], func=ACT.Silu, bias=b1f[:, m : m + 1], scale=1.0
+                    out=hps[g][:, m, :], in_=ps1s[g, m][:], func=ACT.Silu,
+                    bias=b1f[:, m : m + 1], scale=1.0,
                 )
 
-        out_v = out.rearrange("(g a p) o -> g p a o", a=4, p=P)
-        hgs, yts, ps3s, yos = {}, {}, {}, {}
-        for k in range(NG + LV + 1):
+        def regroup_h(g):
+            hgs[g] = gpool.tile([P, 4 * GB], BF16, name="hg", tag="grouped", align_bytes=64)
+            regroup(hgs[g][:], hps[g][:])
+
+        def quantise_h(g):
+            hc = cpool.tile([P, GB], U32, name="hc", align_bytes=64)
+            hs = cpool.tile([P, GB], U8, name="hs", align_bytes=64)
+            hcs[g] = (hc, hs)
+            nc.vector.quantize_mx(out=hc[:].bitcast(FP8X4), scales=hs[:], in_=hgs[g][:])
+
+        def layer2(g):
+            hc, hs = hcs[g]
+            for a in range(2):
+                ps2s[g, a] = mm_bank([P, GB], F32, "ps2")
+                nc.tensor.matmul_mx(
+                    out=ps2s[g, a][:],
+                    lhsT=w2c[:, a * P : (a + 1) * P].bitcast(FP8X4),
+                    lhsT_scale=w2s[:, a * P : (a + 1) * P],
+                    rhs=hc[:].bitcast(FP8X4),
+                    rhs_scale=hs[:],
+                    start=True, stop=True,
+                )
+
+        def silu2(g):
+            yts[g] = ypool.tile([P, 2, GB], F32, name="yt")
+            for a in range(2):
+                nc.scalar.activation(
+                    out=yts[g][:, a, :], in_=ps2s[g, a][:], func=ACT.Silu,
+                    bias=b2f[:, a : a + 1], scale=1.0,
+                )
+
+        def transpose_out(g):
+            for half in range(2):
+                ps3s[g, half] = tr_bank([P, 2, O], F32, "ps3")
+                for j in range(2):
+                    bt = 2 * half + j
+                    for a in range(2):
+                        nc.tensor.transpose(
+                            ps3s[g, half][:, j, a * P : (a + 1) * P],
+                            yts[g][:, a, bt * P : (bt + 1) * P],
+                            ident[:],
+                        )
+
+        def copy_out(g, on_scalar):
+            for half in range(2):
+                if copied_by_scalar(g, half) == on_scalar:
+                    if on_scalar:
+                        y = ypool.tile([P, 2, O], F32, name="ys")
+                        nc.scalar.copy(out=y[:], in_=ps3s[g, half][:])
+                    else:
+                        y = ypool.tile([P, 2, O], F32, name="yv", bufs=6)
+                        nc.vector.tensor_copy(out=y[:], in_=ps3s[g, half][:])
+                    nc.sync.dma_start(out=out_v[g, half], in_=y[:])
+
+        layer1(0)
+        issued2 = 0
+        for k in range(NG + K + 2):
+            g2 = k - K
+            if 0 <= g2 - 1 < NG:
+                transpose_out(g2 - 1)
+            while issued2 < NG and issued2 <= g2:
+                layer2(issued2)
+                issued2 += 1
+            if k + 1 < NG:
+                layer1(k + 1)
+            elif issued2 < NG and issued2 <= g2 + 1:
+                layer2(issued2)
+                issued2 += 1
             if k < NG:
-                hgs[k] = gpool.tile([P, 4 * GB], BF16, name="hg", tag="grouped", align_bytes=64)
-                regroup(hgs[k][:], hps[k][:])
-            g = k - 1
-            if 0 <= g < NG:
-                hc = cpool.tile([P, GB], U32, name="hc", align_bytes=64)
-                hs = cpool.tile([P, GB], U8, name="hs", align_bytes=64)
-                nc.vector.quantize_mx(out=hc[:].bitcast(FP8X4), scales=hs[:], in_=hgs[g][:])
-            gv = k - LV
-            if 0 <= gv < NG:
-                nc.vector.tensor_copy(out=yos[gv][:, 0:2, :], in_=ps3s[gv, 0][:])
-                nc.sync.dma_start(out=out_v[gv], in_=yos[gv][:])
-            if 0 <= g < NG:
-                ps2s = []
-                for a in range(2):
-                    ps2 = psum.tile([P, GB], F32, name="ps2", tag="mm")
-                    nc.tensor.matmul_mx(
-                        out=ps2[:],
-                        lhsT=w2c[:, a * P : (a + 1) * P].bitcast(FP8X4),
-                        lhsT_scale=w2s[:, a * P : (a + 1) * P],
-                        rhs=hc[:].bitcast(FP8X4),
-                        rhs_scale=hs[:],
-                        start=True, stop=True,
-                    )
-                    ps2s.append(ps2)
-            gt = k - 2
-            if 0 <= gt < NG:
-                for half in range(2):
-                    ps3 = psum.tile([P, 2, O], F32, name="ps3", tag="tr")
-                    ps3s[gt, half] = ps3
-                    for j in range(2):
-                        bt = 2 * half + j
-                        for a in range(2):
-                            nc.tensor.transpose(
-                                ps3[:, j, a * P : (a + 1) * P],
-                                yts[gt][:, a, bt * P : (bt + 1) * P],
-                                ident[:],
-                            )
-            if 0 <= g < NG:
-                yts[g] = ypool.tile([P, 2, GB], F32, name="yt")
-                for a in range(2):
-                    nc.scalar.activation(
-                        out=yts[g][:, a, :], in_=ps2s[a][:], func=ACT.Silu,
-                        bias=b2f[:, a : a + 1], scale=1.0,
-                    )
-            if 0 <= gt < NG:
-                yos[gt] = ypool.tile([P, 4, O], F32, name="yo", bufs=5)
-                nc.scalar.copy(out=yos[gt][:, 2:4, :], in_=ps3s[gt, 1][:])
+                silu1(k)
+            if 0 <= g2 < NG:
+                silu2(g2)
+            if 0 <= g2 - 1 < NG:
+                copy_out(g2 - 1, True)
+            if 0 <= k - 1 < NG:
+                regroup_h(k - 1)
+            fills = fill_count(k)
+            if fills > 0:
+                embedding_step()
+            if 0 <= k - 1 < NG:
+                quantise_h(k - 1)
+            if 0 <= g2 - 1 < NG:
+                copy_out(g2 - 1, False)
+            for i in range(fills - 1):
+                embedding_step()

@@ -17,64 +17,51 @@ P = 128
 B, D, H, O = 8192, 512, 512, 256
 FLOPS = 2 * B * D * H + 2 * B * H * O
 
+CB = 1024
+NCH = B // CB
 GB = 512
 NG = B // GB
 FIRST = 256
-TLOAD = 1024
-TC_GROUPS = tuple(range(1, 10))
-N_AHEAD = 12
-K = 4
-N_SCALAR_COPIES = 6
-WPREP_AFTER = 3
-
-
-def fill_count(k):
-    if k < K:
-        return 1
-    return 3 if k == K else 2
+LV = 5
+LS = 1
+WPREP_AFTER = 1
 
 
 def copied_by_scalar(g, half):
-    return half == 1 and (g < N_SCALAR_COPIES or g == NG - 1)
+    return half == 1 or g % 8 == 4
 
 
 def tile_input_timestep_t_kernel(tc, t, W1, b1, W2, b2, out):
     nc = tc.nc
     with ExitStack() as ctx:
         const = ctx.enter_context(tc.tile_pool(name="const", bufs=1))
-        snpool = ctx.enter_context(tc.tile_pool(name="snpool", bufs=8))
+        ring = ctx.enter_context(tc.tile_pool(name="ring", bufs=20))
         epool = ctx.enter_context(tc.tile_pool(name="epool", bufs=2))
-        gpool = ctx.enter_context(tc.tile_pool(name="gpool", bufs=4))
-        hpool = ctx.enter_context(tc.tile_pool(name="hpool", bufs=7))
-        cpool = ctx.enter_context(tc.tile_pool(name="cpool", bufs=4))
+        gpool = ctx.enter_context(tc.tile_pool(name="gpool", bufs=3))
+        cpool = ctx.enter_context(tc.tile_pool(name="cpool", bufs=6))
         ypool = ctx.enter_context(tc.tile_pool(name="ypool", bufs=3))
-        psum = ctx.enter_context(tc.psum_pool(name="psum", bufs=1))
+        psum = ctx.enter_context(tc.psum_pool(name="psum", bufs=4))
         ctx.enter_context(tc.manual_schedule())
 
-        def mm_bank(shape, dtype, name):
-            return psum.tile(shape, dtype, name=name, tag="mm", bufs=5)
-
-        def tr_bank(shape, dtype, name):
-            return psum.tile(shape, dtype, name=name, tag="tr", bufs=3)
+        pieces = [[(0, FIRST), (FIRST, CB)]] + [[(c * CB, (c + 1) * CB)] for c in range(1, NCH)]
 
         tb = const.tile([P, B], BF16, name="tb")
-        cuts = [0, FIRST] + list(range(TLOAD, B + 1, TLOAD))
 
-        def load_t(i):
-            lo, hi = cuts[i], cuts[i + 1]
-            nc.sync.dma_start(out=tb[:, lo:hi], in_=t[lo:hi].partition_broadcast(P))
+        def load_t(c):
+            for lo, hi in pieces[c]:
+                nc.sync.dma_start(out=tb[:, lo:hi], in_=t[lo:hi].partition_broadcast(P))
 
-        for i in range(3):
-            load_t(i)
-        w1raw = hpool.tile([P, 4, D], BF16, name="w1raw", tag="hp", align_bytes=64)
+        load_t(0)
+        load_t(1)
+        w1raw = ring.tile([P, 4, D], BF16, name="w1raw", tag="ring", align_bytes=64)
         nc.sync.dma_start(
             out=w1raw[:].rearrange("p (u e) i -> p u e i", u=2),
             in_=W1.rearrange("(u p e) i -> p u e i", u=2, e=2),
         )
-        w2raw = hpool.tile([P, 2, H], BF16, name="w2raw", tag="hp", align_bytes=64)
+        w2raw = ring.tile([P, 2, H], BF16, name="w2raw", tag="ring", align_bytes=64)
         nc.sync.dma_start(out=w2raw[:], in_=W2.rearrange("(a p) h -> p a h", a=2))
-        for i in range(3, len(cuts) - 1):
-            load_t(i)
+        for c in range(2, NCH):
+            load_t(c)
         b1raw = const.tile([P, 2, 2], BF16, name="b1raw")
         b2raw = const.tile([P, 2], BF16, name="b2raw")
         with nc.allow_non_contiguous_dma(reason="two small bias vectors, one value a partition"):
@@ -83,10 +70,6 @@ def tile_input_timestep_t_kernel(tc, t, W1, b1, W2, b2, out):
 
         idx_i = const.tile([P, 4], I32, name="idx_i")
         nc.gpsimd.iota(idx_i[:], pattern=[[256, 2], [1, 2]], base=0, channel_multiplier=2)
-        xt = const.tile([P, 4, P], BF16, name="xt")
-        nc.gpsimd.memset(xt[:], 0.0)
-        identb = const.tile([P, P], BF16, name="identb")
-        make_identity(nc, identb[:])
         ident = const.tile([P, P], F32, name="ident")
         make_identity(nc, ident[:])
         idx_f = const.tile([P, 4], F32, name="idx_f")
@@ -102,18 +85,6 @@ def tile_input_timestep_t_kernel(tc, t, W1, b1, W2, b2, out):
         nc.scalar.activation(out=csin[:], in_=sbias[:], func=ACT.Sin)
         amp = const.tile([P, 4], F32, name="amp")
         nc.vector.tensor_scalar_mul(out=amp[:], in0=csin[:], scalar1=2.0)
-        rest1 = const.tile([P, 4], F32, name="rest1")
-        rest2 = const.tile([P, 4], F32, name="rest2")
-        nc.vector.tensor_copy(out=xt[:, :, 0], in_=amp[:])
-        nc.vector.tensor_tensor(out=rest1[:], in0=amp[:], in1=xt[:, :, 0], op=ALU.subtract)
-        nc.vector.tensor_copy(out=xt[:, :, 1], in_=rest1[:])
-        nc.vector.tensor_tensor(out=rest2[:], in0=rest1[:], in1=xt[:, :, 1], op=ALU.subtract)
-        nc.vector.tensor_copy(out=xt[:, :, 2], in_=rest2[:])
-        clp = tr_bank([P, 4, P], BF16, "clp")
-        for j in range(4):
-            nc.tensor.transpose(clp[:, j, :], xt[:, j, :], identb[:])
-        cl = const.tile([P, 4, P], BF16, name="cl")
-        nc.vector.tensor_copy(out=cl[:], in_=clp[:])
 
         w1c = const.tile([P, H], U32, name="w1c", align_bytes=64)
         w1s = const.tile([P, H], U8, name="w1s", align_bytes=64)
@@ -123,7 +94,7 @@ def tile_input_timestep_t_kernel(tc, t, W1, b1, W2, b2, out):
         b2f = const.tile([P, 2], F32, name="b2f")
         wts = []
         for a in range(3):
-            wt = mm_bank([P, 2, 2, P], F32, "wt")
+            wt = psum.tile([P, 2, 2, P], F32, name="wt", tag="mm")
             for m in range(2):
                 src = w1raw[:, 2 * a + m, :] if a < 2 else w2raw[:, m, :]
                 for u in range(2):
@@ -133,8 +104,8 @@ def tile_input_timestep_t_kernel(tc, t, W1, b1, W2, b2, out):
             wts.append(wt)
 
         def weight_prep():
-            w1g = hpool.tile([P, 4, P, 4], BF16, name="w1g", tag="hp", align_bytes=64)
-            w2g = hpool.tile([P, 2, P, 4], BF16, name="w2g", tag="hp", align_bytes=64)
+            w1g = ring.tile([P, 4, P, 4], BF16, name="w1g", tag="ring", align_bytes=64)
+            w2g = ring.tile([P, 2, P, 4], BF16, name="w2g", tag="ring", align_bytes=64)
             w1gw = w1g[:].bitcast(F32)
             for a in range(2):
                 nc.vector.tensor_copy(
@@ -163,193 +134,105 @@ def tile_input_timestep_t_kernel(tc, t, W1, b1, W2, b2, out):
 
         ec = const.tile([P, B], U32, name="ec", align_bytes=64)
         es = const.tile([P, B], U8, name="es", align_bytes=64)
-        sns, eps, egs = {}, {}, {}
-
-        def pieces_of(g):
-            return [(0, FIRST), (FIRST, GB)] if g == 0 else [(0, GB)]
-
-        def sines(g):
-            sns[g] = snpool.tile([P, 4, GB], F32, name="sn")
-            for lo, hi in pieces_of(g):
+        for c in range(NCH):
+            ep = epool.tile([P, 4, CB], BF16, name="ep")
+            for lo, hi in pieces[c]:
                 for m in range(4):
+                    sn = ring.tile([P, CB], F32, name="sn", tag="ring", align_bytes=64)
                     nc.scalar.activation(
-                        out=sns[g][:, m, lo:hi], in_=tb[:, g * GB + lo : g * GB + hi], func=ACT.Sin,
+                        out=sn[:, 0 : hi - lo], in_=tb[:, lo:hi], func=ACT.Sin,
                         bias=sbias[:, m : m + 1], scale=negphi[:, m : m + 1],
                     )
-
-        def grouped_tile(g):
-            egs[g] = gpool.tile([P, 4 * GB], BF16, name="eg", tag="grouped", align_bytes=64)
-
-        def amplitude_plane(g, lo, hi, m):
-            if g not in eps:
-                eps[g] = epool.tile([P, 4, GB], BF16, name="ep")
-            nc.vector.scalar_tensor_tensor(
-                out=eps[g][:, m, lo:hi], in0=sns[g][:, m, lo:hi], scalar=amp[:, m : m + 1],
-                in1=tb[:, g * GB + lo : g * GB + hi], op0=ALU.mult, op1=ALU.mult,
-            )
-
-        def regroup_embedding(g):
-            grouped_tile(g)
-            regroup(egs[g][:], eps[g][:])
-
-        def amplitude_grouped(g, q):
-            if q == 0:
-                grouped_tile(g)
-            bank = tr_bank([P, 4, P], F32, "tcb")
-            cols = slice(g * GB + q * P, g * GB + (q + 1) * P)
-            for j in range(4):
-                nc.tensor.matmul(
-                    out=bank[:, j, :], lhsT=cl[:, j, :], rhs=tb[:, cols], start=True, stop=True
+                    nc.vector.scalar_tensor_tensor(
+                        out=ep[:, m, lo - c * CB : hi - c * CB], in0=sn[:, 0 : hi - lo],
+                        scalar=amp[:, m : m + 1], in1=tb[:, lo:hi],
+                        op0=ALU.mult, op1=ALU.mult,
+                    )
+            egs = []
+            for s in range(2):
+                eg = gpool.tile([P, 4 * GB], BF16, name="eg", tag="grouped", align_bytes=64)
+                regroup(eg[:], ep[:, :, s * GB : (s + 1) * GB])
+                egs.append(eg)
+            for s in range(2):
+                half = slice(c * CB + s * GB, c * CB + (s + 1) * GB)
+                nc.vector.quantize_mx(
+                    out=ec[:, half].bitcast(FP8X4), scales=es[:, half], in_=egs[s][:]
                 )
-            nc.vector.tensor_tensor(
-                out=egs[g][:, q * 4 * P : (q + 1) * 4 * P].rearrange("p (b j) -> p b j", j=4),
-                in0=bank[:].rearrange("p j b -> p b j"),
-                in1=sns[g][:, :, q * P : (q + 1) * P].rearrange("p j b -> p b j"),
-                op=ALU.mult,
-            )
+            if c == WPREP_AFTER:
+                weight_prep()
 
-        def quantise_embedding(g):
-            cols = slice(g * GB, (g + 1) * GB)
-            nc.vector.quantize_mx(out=ec[:, cols].bitcast(FP8X4), scales=es[:, cols], in_=egs[g][:])
-
-        stream = []
+        hps = []
         for g in range(NG):
-            if g in TC_GROUPS:
-                work = [(g, amplitude_grouped, (g, q)) for q in range(4)]
-            else:
-                work = [
-                    (g, amplitude_plane, (g, lo, hi, m)) for lo, hi in pieces_of(g) for m in range(4)
-                ] + [(g, regroup_embedding, (g,))]
-            stream.append(work[0])
-            if g > 0:
-                stream.append((g, quantise_embedding, (g - 1,)))
-            stream.extend(work[1:])
-            if g == WPREP_AFTER:
-                stream.append((g, weight_prep, ()))
-        stream.append((NG - 1, quantise_embedding, (NG - 1,)))
-        position = [0]
-
-        def embedding_step():
-            if position[0] < len(stream):
-                g, call, args = stream[position[0]]
-                position[0] += 1
-                if g not in sns:
-                    sines(g)
-                call(*args)
-
-        ahead = stream.index((N_AHEAD, quantise_embedding, (N_AHEAD - 1,))) + 1
-        for i in range(ahead):
-            embedding_step()
-        for g in range(NG):
-            if g not in sns:
-                sines(g)
-
-        out_v = out.rearrange("(g s a p) o -> g s p a o", s=2, a=2, p=P)
-        ps1s, hps, hgs, hcs, ps2s, yts, ps3s = {}, {}, {}, {}, {}, {}, {}
-
-        def layer1(g):
             cols = slice(g * GB, (g + 1) * GB)
+            hp = ring.tile([P, 4, GB], BF16, name="hp", tag="ring", align_bytes=64)
+            hps.append(hp)
             for m in range(4):
-                ps1s[g, m] = mm_bank([P, GB], F32, "ps1")
+                ps1 = psum.tile([P, GB], F32, name="ps1", tag="mm")
                 nc.tensor.matmul_mx(
-                    out=ps1s[g, m][:],
+                    out=ps1[:],
                     lhsT=w1c[:, m * P : (m + 1) * P].bitcast(FP8X4),
                     lhsT_scale=w1s[:, m * P : (m + 1) * P],
                     rhs=ec[:, cols].bitcast(FP8X4),
                     rhs_scale=es[:, cols],
                     start=True, stop=True,
                 )
-
-        def silu1(g):
-            hps[g] = hpool.tile([P, 4, GB], BF16, name="hp", tag="hp", align_bytes=64)
-            for m in range(4):
                 nc.scalar.activation(
-                    out=hps[g][:, m, :], in_=ps1s[g, m][:], func=ACT.Silu,
-                    bias=b1f[:, m : m + 1], scale=1.0,
+                    out=hp[:, m, :], in_=ps1[:], func=ACT.Silu, bias=b1f[:, m : m + 1], scale=1.0
                 )
 
-        def regroup_h(g):
-            hgs[g] = gpool.tile([P, 4 * GB], BF16, name="hg", tag="grouped", align_bytes=64)
-            regroup(hgs[g][:], hps[g][:])
-
-        def quantise_h(g):
-            hc = cpool.tile([P, GB], U32, name="hc", align_bytes=64)
-            hs = cpool.tile([P, GB], U8, name="hs", align_bytes=64)
-            hcs[g] = (hc, hs)
-            nc.vector.quantize_mx(out=hc[:].bitcast(FP8X4), scales=hs[:], in_=hgs[g][:])
-
-        def layer2(g):
-            hc, hs = hcs[g]
-            for a in range(2):
-                ps2s[g, a] = mm_bank([P, GB], F32, "ps2")
-                nc.tensor.matmul_mx(
-                    out=ps2s[g, a][:],
-                    lhsT=w2c[:, a * P : (a + 1) * P].bitcast(FP8X4),
-                    lhsT_scale=w2s[:, a * P : (a + 1) * P],
-                    rhs=hc[:].bitcast(FP8X4),
-                    rhs_scale=hs[:],
-                    start=True, stop=True,
-                )
-
-        def silu2(g):
-            yts[g] = ypool.tile([P, 2, GB], F32, name="yt")
-            for a in range(2):
-                nc.scalar.activation(
-                    out=yts[g][:, a, :], in_=ps2s[g, a][:], func=ACT.Silu,
-                    bias=b2f[:, a : a + 1], scale=1.0,
-                )
-
-        def transpose_out(g):
-            for half in range(2):
-                ps3s[g, half] = tr_bank([P, 2, O], F32, "ps3")
-                for j in range(2):
-                    bt = 2 * half + j
-                    for a in range(2):
-                        nc.tensor.transpose(
-                            ps3s[g, half][:, j, a * P : (a + 1) * P],
-                            yts[g][:, a, bt * P : (bt + 1) * P],
-                            ident[:],
-                        )
-
-        def copy_out(g, on_scalar):
-            for half in range(2):
-                if copied_by_scalar(g, half) == on_scalar:
-                    if on_scalar:
-                        y = ypool.tile([P, 2, O], F32, name="ys")
-                        nc.scalar.copy(out=y[:], in_=ps3s[g, half][:])
-                    else:
-                        y = ypool.tile([P, 2, O], F32, name="yv", bufs=6)
-                        nc.vector.tensor_copy(out=y[:], in_=ps3s[g, half][:])
-                    nc.sync.dma_start(out=out_v[g, half], in_=y[:])
-
-        layer1(0)
-        issued2 = 0
-        for k in range(NG + K + 2):
-            g2 = k - K
-            if 0 <= g2 - 1 < NG:
-                transpose_out(g2 - 1)
-            while issued2 < NG and issued2 <= g2:
-                layer2(issued2)
-                issued2 += 1
-            if k + 1 < NG:
-                layer1(k + 1)
-            elif issued2 < NG and issued2 <= g2 + 1:
-                layer2(issued2)
-                issued2 += 1
+        out_v = out.rearrange("(g s a p) o -> g s p a o", s=2, a=2, p=P)
+        hgs, yts, ps3s = {}, {}, {}
+        for k in range(NG + LV + 1):
             if k < NG:
-                silu1(k)
-            if 0 <= g2 < NG:
-                silu2(g2)
-            if 0 <= g2 - 1 < NG:
-                copy_out(g2 - 1, True)
-            if 0 <= k - 1 < NG:
-                regroup_h(k - 1)
-            fills = fill_count(k)
-            if fills > 0:
-                embedding_step()
-            if 0 <= k - 1 < NG:
-                quantise_h(k - 1)
-            if 0 <= g2 - 1 < NG:
-                copy_out(g2 - 1, False)
-            for i in range(fills - 1):
-                embedding_step()
+                hgs[k] = gpool.tile([P, 4 * GB], BF16, name="hg", tag="grouped", align_bytes=64)
+                regroup(hgs[k][:], hps[k][:])
+            g = k - 1
+            if 0 <= g < NG:
+                hc = cpool.tile([P, GB], U32, name="hc", align_bytes=64)
+                hs = cpool.tile([P, GB], U8, name="hs", align_bytes=64)
+                nc.vector.quantize_mx(out=hc[:].bitcast(FP8X4), scales=hs[:], in_=hgs[g][:])
+            gv = k - LV
+            if 0 <= gv < NG and not copied_by_scalar(gv, 0):
+                yv = ypool.tile([P, 2, O], F32, name="yv", bufs=6)
+                nc.vector.tensor_copy(out=yv[:], in_=ps3s[gv, 0][:])
+                nc.sync.dma_start(out=out_v[gv, 0], in_=yv[:])
+            if 0 <= g < NG:
+                ps2s = []
+                for a in range(2):
+                    ps2 = psum.tile([P, GB], F32, name="ps2", tag="mm")
+                    nc.tensor.matmul_mx(
+                        out=ps2[:],
+                        lhsT=w2c[:, a * P : (a + 1) * P].bitcast(FP8X4),
+                        lhsT_scale=w2s[:, a * P : (a + 1) * P],
+                        rhs=hc[:].bitcast(FP8X4),
+                        rhs_scale=hs[:],
+                        start=True, stop=True,
+                    )
+                    ps2s.append(ps2)
+            gt = k - 2
+            if 0 <= gt < NG:
+                for half in range(2):
+                    ps3 = psum.tile([P, 2, O], F32, name="ps3", tag="tr")
+                    ps3s[gt, half] = ps3
+                    for j in range(2):
+                        bt = 2 * half + j
+                        for a in range(2):
+                            nc.tensor.transpose(
+                                ps3[:, j, a * P : (a + 1) * P],
+                                yts[gt][:, a, bt * P : (bt + 1) * P],
+                                ident[:],
+                            )
+            if 0 <= g < NG:
+                yts[g] = ypool.tile([P, 2, GB], F32, name="yt")
+                for a in range(2):
+                    nc.scalar.activation(
+                        out=yts[g][:, a, :], in_=ps2s[a][:], func=ACT.Silu,
+                        bias=b2f[:, a : a + 1], scale=1.0,
+                    )
+            gs = k - 1 - LS
+            if 0 <= gs < NG:
+                for half in range(2):
+                    if copied_by_scalar(gs, half):
+                        ys = ypool.tile([P, 2, O], F32, name="ys", bufs=6)
+                        nc.scalar.copy(out=ys[:], in_=ps3s[gs, half][:])
+                        nc.sync.dma_start(out=out_v[gs, half], in_=ys[:])

@@ -28,7 +28,7 @@ WPREP_AFTER = 1
 
 
 def copied_by_scalar(g, half):
-    return half == 1 or g % 8 == 4
+    return g % 2 == 1 or g == 8
 
 
 def tile_input_timestep_t_kernel(tc, t, W1, b1, W2, b2, out):
@@ -192,10 +192,12 @@ def tile_input_timestep_t_kernel(tc, t, W1, b1, W2, b2, out):
                 hs = cpool.tile([P, GB], U8, name="hs", align_bytes=64)
                 nc.vector.quantize_mx(out=hc[:].bitcast(FP8X4), scales=hs[:], in_=hgs[g][:])
             gv = k - LV
-            if 0 <= gv < NG and not copied_by_scalar(gv, 0):
-                yv = ypool.tile([P, 2, O], F32, name="yv", bufs=6)
-                nc.vector.tensor_copy(out=yv[:], in_=ps3s[gv, 0][:])
-                nc.sync.dma_start(out=out_v[gv, 0], in_=yv[:])
+            if 0 <= gv < NG:
+                for half in range(2):
+                    if not copied_by_scalar(gv, half):
+                        yv = ypool.tile([P, 2, O], F32, name="yv", bufs=6)
+                        nc.vector.tensor_copy(out=yv[:], in_=ps3s[gv, half][:])
+                        nc.sync.dma_start(out=out_v[gv, half], in_=yv[:])
             if 0 <= g < NG:
                 ps2s = []
                 for a in range(2):

@@ -25,6 +25,9 @@ FIRST = 256
 LV = 5
 LS = 1
 WPREP_AFTER = 1
+GT = 768
+GPIECE = 256
+TBA = 4
 
 
 def copied_by_scalar(g, half):
@@ -38,6 +41,7 @@ def tile_input_timestep_t_kernel(tc, t, W1, b1, W2, b2, out):
         ring = ctx.enter_context(tc.tile_pool(name="ring", bufs=20))
         epool = ctx.enter_context(tc.tile_pool(name="epool", bufs=2))
         gpool = ctx.enter_context(tc.tile_pool(name="gpool", bufs=3))
+        egpool = ctx.enter_context(tc.tile_pool(name="egpool", bufs=1))
         cpool = ctx.enter_context(tc.tile_pool(name="cpool", bufs=6))
         ypool = ctx.enter_context(tc.tile_pool(name="ypool", bufs=3))
         psum = ctx.enter_context(tc.psum_pool(name="psum", bufs=4))
@@ -51,7 +55,13 @@ def tile_input_timestep_t_kernel(tc, t, W1, b1, W2, b2, out):
             for lo, hi in pieces[c]:
                 nc.sync.dma_start(out=tb[:, lo:hi], in_=t[lo:hi].partition_broadcast(P))
 
-        load_t(0)
+        t16 = const.tile([P, GB], BF16, name="t16")
+        nc.vector.memset(t16[:], 0.0)
+        lo0, hi0 = pieces[0][0]
+        nc.sync.dma_start(out=tb[:, lo0:hi0], in_=t[lo0:hi0].partition_broadcast(P))
+        nc.sync.dma_start(out=t16[0:NG, :], in_=t.rearrange("(g n) -> g n", n=GB))
+        lo1, hi1 = pieces[0][1]
+        nc.sync.dma_start(out=tb[:, lo1:hi1], in_=t[lo1:hi1].partition_broadcast(P))
         load_t(1)
         w1raw = ring.tile([P, 4, D], BF16, name="w1raw", tag="ring", align_bytes=64)
         nc.sync.dma_start(
@@ -81,10 +91,28 @@ def tile_input_timestep_t_kernel(tc, t, W1, b1, W2, b2, out):
             out=sbias[:], in0=idx_f[:], scalar1=math.pi / (2 * D), scalar2=math.pi / 4,
             op0=ALU.mult, op1=ALU.add,
         )
+        identb = const.tile([P, P], BF16, name="identb")
+        nc.vector.tensor_copy(out=identb[:], in_=ident[:])
         csin = const.tile([P, 4], F32, name="csin")
         nc.scalar.activation(out=csin[:], in_=sbias[:], func=ACT.Sin)
         amp = const.tile([P, 4], F32, name="amp")
         nc.vector.tensor_scalar_mul(out=amp[:], in0=csin[:], scalar1=2.0)
+
+        tbps = {}
+
+        def broadcast_t(c):
+            tbp = psum.tile([P, CB], BF16, name="tbp", tag="tr")
+            tbps[c] = tbp
+            for s in range(2):
+                g = 2 * c + s
+                nc.tensor.matmul(
+                    out=tbp[:, s * GB : (s + 1) * GB],
+                    lhsT=identb[:, g : g + 1].to_broadcast([P, P]),
+                    rhs=t16[:], start=True, stop=True,
+                )
+
+        for c in range(TBA):
+            broadcast_t(c)
 
         w1c = const.tile([P, H], U32, name="w1c", align_bytes=64)
         w1s = const.tile([P, H], U8, name="w1s", align_bytes=64)
@@ -134,32 +162,43 @@ def tile_input_timestep_t_kernel(tc, t, W1, b1, W2, b2, out):
 
         ec = const.tile([P, B], U32, name="ec", align_bytes=64)
         es = const.tile([P, B], U8, name="es", align_bytes=64)
-        for c in range(NCH):
-            ep = epool.tile([P, 4, CB], BF16, name="ep")
-            for lo, hi in pieces[c]:
-                for m in range(4):
-                    sn = ring.tile([P, CB], F32, name="sn", tag="ring", align_bytes=64)
-                    nc.scalar.activation(
-                        out=sn[:, 0 : hi - lo], in_=tb[:, lo:hi], func=ACT.Sin,
-                        bias=sbias[:, m : m + 1], scale=negphi[:, m : m + 1],
+        eps = {}
+        for c in range(NCH + 1):
+            if c < NCH:
+                ep = epool.tile([P, 4, CB], BF16, name="ep")
+                eps[c] = ep
+                for lo, hi in pieces[c]:
+                    for m in range(4):
+                        sn = ring.tile([P, CB], F32, name="sn", tag="ring", align_bytes=64)
+                        nc.scalar.activation(
+                            out=sn[:, 0 : hi - lo], in_=tb[:, lo:hi], func=ACT.Sin,
+                            bias=sbias[:, m : m + 1], scale=negphi[:, m : m + 1],
+                        )
+                        nc.vector.scalar_tensor_tensor(
+                            out=ep[:, m, lo - c * CB : hi - c * CB], in0=sn[:, 0 : hi - lo],
+                            scalar=amp[:, m : m + 1], in1=tbps[c][:, lo - c * CB : hi - c * CB],
+                            op0=ALU.mult, op1=ALU.mult,
+                        )
+                if c + TBA < NCH:
+                    broadcast_t(c + TBA)
+            d = c - 1
+            if d >= 0:
+                eg = egpool.tile([P, 4 * CB], BF16, name="eg", align_bytes=64)
+                for q in range(0, GT, GPIECE):
+                    nc.gpsimd.tensor_scalar(
+                        out=eg[:, 4 * q : 4 * (q + GPIECE)].rearrange("p (c k) -> p c k", k=4),
+                        in0=eps[d][:, :, q : q + GPIECE].rearrange("p k c -> p c k"),
+                        scalar1=1.0, scalar2=0.0, op0=ALU.mult, op1=ALU.add,
                     )
-                    nc.vector.scalar_tensor_tensor(
-                        out=ep[:, m, lo - c * CB : hi - c * CB], in0=sn[:, 0 : hi - lo],
-                        scalar=amp[:, m : m + 1], in1=tb[:, lo:hi],
-                        op0=ALU.mult, op1=ALU.mult,
+                regroup(eg[:, 4 * GT :], eps[d][:, :, GT:])
+                if d == WPREP_AFTER:
+                    weight_prep()
+                for s in range(2):
+                    half = slice(d * CB + s * GB, d * CB + (s + 1) * GB)
+                    nc.vector.quantize_mx(
+                        out=ec[:, half].bitcast(FP8X4), scales=es[:, half],
+                        in_=eg[:, s * 4 * GB : (s + 1) * 4 * GB],
                     )
-            egs = []
-            for s in range(2):
-                eg = gpool.tile([P, 4 * GB], BF16, name="eg", tag="grouped", align_bytes=64)
-                regroup(eg[:], ep[:, :, s * GB : (s + 1) * GB])
-                egs.append(eg)
-            for s in range(2):
-                half = slice(c * CB + s * GB, c * CB + (s + 1) * GB)
-                nc.vector.quantize_mx(
-                    out=ec[:, half].bitcast(FP8X4), scales=es[:, half], in_=egs[s][:]
-                )
-            if c == WPREP_AFTER:
-                weight_prep()
 
         hps = []
         for g in range(NG):

@@ -28,10 +28,12 @@ WPREP_AFTER = 1
 GT = 768
 GPIECE = 256
 TBA = 4
+PRE = 40
+RATE = 2
 
 
 def copied_by_scalar(g, half):
-    return g % 2 == 1 or g == 8
+    return (g % 4 == 3 and g != NG - 1) or (g == NG - 1 and half == 1)
 
 
 def tile_input_timestep_t_kernel(tc, t, W1, b1, W2, b2, out):
@@ -200,28 +202,34 @@ def tile_input_timestep_t_kernel(tc, t, W1, b1, W2, b2, out):
                         in_=eg[:, s * 4 * GB : (s + 1) * 4 * GB],
                     )
 
-        hps = []
-        for g in range(NG):
+        hps = {}
+
+        def layer1_tile(i):
+            g, m = divmod(i, 4)
             cols = slice(g * GB, (g + 1) * GB)
-            hp = ring.tile([P, 4, GB], BF16, name="hp", tag="ring", align_bytes=64)
-            hps.append(hp)
-            for m in range(4):
-                ps1 = psum.tile([P, GB], F32, name="ps1", tag="mm")
-                nc.tensor.matmul_mx(
-                    out=ps1[:],
-                    lhsT=w1c[:, m * P : (m + 1) * P].bitcast(FP8X4),
-                    lhsT_scale=w1s[:, m * P : (m + 1) * P],
-                    rhs=ec[:, cols].bitcast(FP8X4),
-                    rhs_scale=es[:, cols],
-                    start=True, stop=True,
-                )
-                nc.scalar.activation(
-                    out=hp[:, m, :], in_=ps1[:], func=ACT.Silu, bias=b1f[:, m : m + 1], scale=1.0
-                )
+            if m == 0:
+                hps[g] = ring.tile([P, 4, GB], BF16, name="hp", tag="ring", align_bytes=64)
+            ps1 = psum.tile([P, GB], F32, name="ps1", tag="mm")
+            nc.tensor.matmul_mx(
+                out=ps1[:],
+                lhsT=w1c[:, m * P : (m + 1) * P].bitcast(FP8X4),
+                lhsT_scale=w1s[:, m * P : (m + 1) * P],
+                rhs=ec[:, cols].bitcast(FP8X4),
+                rhs_scale=es[:, cols],
+                start=True, stop=True,
+            )
+            nc.scalar.activation(
+                out=hps[g][:, m, :], in_=ps1[:], func=ACT.Silu, bias=b1f[:, m : m + 1], scale=1.0
+            )
+
+        for i in range(PRE):
+            layer1_tile(i)
 
         out_v = out.rearrange("(g s a p) o -> g s p a o", s=2, a=2, p=P)
         hgs, yts, ps3s = {}, {}, {}
         for k in range(NG + LV + 1):
+            for i in range(PRE + RATE * k, min(PRE + RATE * (k + 1), 4 * NG)):
+                layer1_tile(i)
             if k < NG:
                 hgs[k] = gpool.tile([P, 4 * GB], BF16, name="hg", tag="grouped", align_bytes=64)
                 regroup(hgs[k][:], hps[k][:])

@@ -22,18 +22,15 @@ NCH = B // CB
 GB = 512
 NG = B // GB
 FIRST = 256
-LV = 5
-LS = 1
+LADD = 2
+LSIL = 3
 WPREP_AFTER = 1
 GT = 768
 GPIECE = 256
 TBA = 4
 PRE = 40
 RATE = 2
-
-
-def copied_by_scalar(g, half):
-    return (g % 4 == 3 and g != NG - 1) or (g == NG - 1 and half == 1)
+GH = 192
 
 
 def tile_input_timestep_t_kernel(tc, t, W1, b1, W2, b2, out):
@@ -42,11 +39,11 @@ def tile_input_timestep_t_kernel(tc, t, W1, b1, W2, b2, out):
         const = ctx.enter_context(tc.tile_pool(name="const", bufs=1))
         ring = ctx.enter_context(tc.tile_pool(name="ring", bufs=20))
         epool = ctx.enter_context(tc.tile_pool(name="epool", bufs=2))
-        gpool = ctx.enter_context(tc.tile_pool(name="gpool", bufs=3))
         egpool = ctx.enter_context(tc.tile_pool(name="egpool", bufs=1))
+        hgpool = ctx.enter_context(tc.tile_pool(name="hgpool", bufs=2))
         cpool = ctx.enter_context(tc.tile_pool(name="cpool", bufs=6))
-        ypool = ctx.enter_context(tc.tile_pool(name="ypool", bufs=3))
-        psum = ctx.enter_context(tc.psum_pool(name="psum", bufs=4))
+        zpool = ctx.enter_context(tc.tile_pool(name="zpool", bufs=4))
+        psum = ctx.enter_context(tc.psum_pool(name="psum", bufs=8))
         ctx.enter_context(tc.manual_schedule())
 
         pieces = [[(0, FIRST), (FIRST, CB)]] + [[(c * CB, (c + 1) * CB)] for c in range(1, NCH)]
@@ -75,10 +72,10 @@ def tile_input_timestep_t_kernel(tc, t, W1, b1, W2, b2, out):
         for c in range(2, NCH):
             load_t(c)
         b1raw = const.tile([P, 2, 2], BF16, name="b1raw")
-        b2raw = const.tile([P, 2], BF16, name="b2raw")
+        b2raw = const.tile([P, O], BF16, name="b2raw")
         with nc.allow_non_contiguous_dma(reason="two small bias vectors, one value a partition"):
             nc.sync.dma_start(out=b1raw[:], in_=b1.rearrange("(u p e) -> p u e", u=2, e=2))
-            nc.sync.dma_start(out=b2raw[:], in_=b2.rearrange("(a p) -> p a", a=2))
+        nc.sync.dma_start(out=b2raw[:], in_=b2.partition_broadcast(P))
 
         idx_i = const.tile([P, 4], I32, name="idx_i")
         nc.gpsimd.iota(idx_i[:], pattern=[[256, 2], [1, 2]], base=0, channel_multiplier=2)
@@ -103,7 +100,7 @@ def tile_input_timestep_t_kernel(tc, t, W1, b1, W2, b2, out):
         tbps = {}
 
         def broadcast_t(c):
-            tbp = psum.tile([P, CB], BF16, name="tbp", tag="tr")
+            tbp = psum.tile([P, CB], BF16, name="tbp", tag="bank")
             tbps[c] = tbp
             for s in range(2):
                 g = 2 * c + s
@@ -121,10 +118,10 @@ def tile_input_timestep_t_kernel(tc, t, W1, b1, W2, b2, out):
         w2c = const.tile([P, O], U32, name="w2c", align_bytes=64)
         w2s = const.tile([P, O], U8, name="w2s", align_bytes=64)
         b1f = const.tile([P, 4], F32, name="b1f")
-        b2f = const.tile([P, 2], F32, name="b2f")
+        b2f = const.tile([P, 2, O], F32, name="b2f")
         wts = []
         for a in range(3):
-            wt = psum.tile([P, 2, 2, P], F32, name="wt", tag="mm")
+            wt = psum.tile([P, 2, 2, P], F32, name="wt", tag="bank")
             for m in range(2):
                 src = w1raw[:, 2 * a + m, :] if a < 2 else w2raw[:, m, :]
                 for u in range(2):
@@ -154,7 +151,8 @@ def tile_input_timestep_t_kernel(tc, t, W1, b1, W2, b2, out):
                 in_=w2g[:].rearrange("p m h k -> p (m h k)"),
             )
             nc.vector.tensor_copy(out=b1f[:], in_=b1raw[:].rearrange("p u e -> p (u e)"))
-            nc.vector.tensor_copy(out=b2f[:], in_=b2raw[:])
+            for j in range(2):
+                nc.vector.tensor_copy(out=b2f[:, j, :], in_=b2raw[:])
 
         def regroup(dst, src):
             nc.vector.tensor_copy(
@@ -209,7 +207,7 @@ def tile_input_timestep_t_kernel(tc, t, W1, b1, W2, b2, out):
             cols = slice(g * GB, (g + 1) * GB)
             if m == 0:
                 hps[g] = ring.tile([P, 4, GB], BF16, name="hp", tag="ring", align_bytes=64)
-            ps1 = psum.tile([P, GB], F32, name="ps1", tag="mm")
+            ps1 = psum.tile([P, GB], F32, name="ps1", tag="bank")
             nc.tensor.matmul_mx(
                 out=ps1[:],
                 lhsT=w1c[:, m * P : (m + 1) * P].bitcast(FP8X4),
@@ -225,63 +223,54 @@ def tile_input_timestep_t_kernel(tc, t, W1, b1, W2, b2, out):
         for i in range(PRE):
             layer1_tile(i)
 
-        out_v = out.rearrange("(g s a p) o -> g s p a o", s=2, a=2, p=P)
-        hgs, yts, ps3s = {}, {}, {}
-        for k in range(NG + LV + 1):
+        out_v = out.rearrange("(g a p) o -> g p a o", a=4, p=P)
+        hgs, hcs, hss, ps2s, zs = {}, {}, {}, {}, {}
+        for k in range(NG + LSIL + 1):
             for i in range(PRE + RATE * k, min(PRE + RATE * (k + 1), 4 * NG)):
                 layer1_tile(i)
             if k < NG:
-                hgs[k] = gpool.tile([P, 4 * GB], BF16, name="hg", tag="grouped", align_bytes=64)
-                regroup(hgs[k][:], hps[k][:])
+                if k in hgs:
+                    regroup(hgs[k][:, 4 * GH :], hps[k][:, :, GH:])
+                else:
+                    hgs[k] = hgpool.tile([P, 4 * GB], BF16, name="hg", align_bytes=64)
+                    regroup(hgs[k][:], hps[k][:])
             g = k - 1
             if 0 <= g < NG:
-                hc = cpool.tile([P, GB], U32, name="hc", align_bytes=64)
-                hs = cpool.tile([P, GB], U8, name="hs", align_bytes=64)
-                nc.vector.quantize_mx(out=hc[:].bitcast(FP8X4), scales=hs[:], in_=hgs[g][:])
-            gv = k - LV
-            if 0 <= gv < NG:
-                for half in range(2):
-                    if not copied_by_scalar(gv, half):
-                        yv = ypool.tile([P, 2, O], F32, name="yv", bufs=6)
-                        nc.vector.tensor_copy(out=yv[:], in_=ps3s[gv, half][:])
-                        nc.sync.dma_start(out=out_v[gv, half], in_=yv[:])
-            if 0 <= g < NG:
-                ps2s = []
-                for a in range(2):
-                    ps2 = psum.tile([P, GB], F32, name="ps2", tag="mm")
-                    nc.tensor.matmul_mx(
-                        out=ps2[:],
-                        lhsT=w2c[:, a * P : (a + 1) * P].bitcast(FP8X4),
-                        lhsT_scale=w2s[:, a * P : (a + 1) * P],
-                        rhs=hc[:].bitcast(FP8X4),
-                        rhs_scale=hs[:],
-                        start=True, stop=True,
-                    )
-                    ps2s.append(ps2)
-            gt = k - 2
-            if 0 <= gt < NG:
-                for half in range(2):
-                    ps3 = psum.tile([P, 2, O], F32, name="ps3", tag="tr")
-                    ps3s[gt, half] = ps3
+                hcs[g] = cpool.tile([P, GB], U32, name="hc", align_bytes=64)
+                hss[g] = cpool.tile([P, GB], U8, name="hs", align_bytes=64)
+                nc.vector.quantize_mx(out=hcs[g][:].bitcast(FP8X4), scales=hss[g][:], in_=hgs[g][:])
+                for s in range(2):
+                    ps2 = psum.tile([P, 2, O], F32, name="ps2", tag="bank")
+                    ps2s[g, s] = ps2
                     for j in range(2):
-                        bt = 2 * half + j
-                        for a in range(2):
-                            nc.tensor.transpose(
-                                ps3[:, j, a * P : (a + 1) * P],
-                                yts[gt][:, a, bt * P : (bt + 1) * P],
-                                ident[:],
-                            )
-            if 0 <= g < NG:
-                yts[g] = ypool.tile([P, 2, GB], F32, name="yt")
-                for a in range(2):
-                    nc.scalar.activation(
-                        out=yts[g][:, a, :], in_=ps2s[a][:], func=ACT.Silu,
-                        bias=b2f[:, a : a + 1], scale=1.0,
+                        bt = 2 * s + j
+                        nc.tensor.matmul_mx(
+                            out=ps2[:, j, :],
+                            lhsT=hcs[g][:, bt * P : (bt + 1) * P].bitcast(FP8X4),
+                            lhsT_scale=hss[g][:, bt * P : (bt + 1) * P],
+                            rhs=w2c[:].bitcast(FP8X4),
+                            rhs_scale=w2s[:],
+                            start=True, stop=True,
+                        )
+            ga = k - LADD
+            if 0 <= ga < NG and k + 1 < NG:
+                hgs[k + 1] = hgpool.tile([P, 4 * GB], BF16, name="hg", align_bytes=64)
+                nc.gpsimd.tensor_scalar(
+                    out=hgs[k + 1][:, 0 : 4 * GH].rearrange("p (c k) -> p c k", k=4),
+                    in0=hps[k + 1][:, :, 0:GH].rearrange("p k c -> p c k"),
+                    scalar1=1.0, scalar2=0.0, op0=ALU.mult, op1=ALU.add,
+                )
+            if 0 <= ga < NG:
+                zs[ga] = zpool.tile([P, 4, O], F32, name="z")
+                for s in range(2):
+                    nc.vector.tensor_tensor(
+                        out=zs[ga][:, 2 * s : 2 * s + 2, :], in0=ps2s[ga, s][:], in1=b2f[:], op=ALU.add
                     )
-            gs = k - 1 - LS
+            gs = k - LSIL
             if 0 <= gs < NG:
-                for half in range(2):
-                    if copied_by_scalar(gs, half):
-                        ys = ypool.tile([P, 2, O], F32, name="ys", bufs=6)
-                        nc.scalar.copy(out=ys[:], in_=ps3s[gs, half][:])
-                        nc.sync.dma_start(out=out_v[gs, half], in_=ys[:])
+                parts = 2 if gs == NG - 1 else 1
+                w = 4 // parts
+                for s in range(parts):
+                    zz = zs[gs][:, s * w : (s + 1) * w, :]
+                    nc.scalar.activation(out=zz, in_=zz, func=ACT.Silu)
+                    nc.sync.dma_start(out=out_v[gs][:, s * w : (s + 1) * w, :], in_=zz)

@@ -26,11 +26,11 @@ LADD = 2
 LSIL = 3
 WPREP_AFTER = 1
 GT = 768
-GPIECE = 256
+GPIECE = 768
 TBA = 4
 PRE = 40
 RATE = 2
-GH = 192
+GH = 128
 
 
 def tile_input_timestep_t_kernel(tc, t, W1, b1, W2, b2, out):

@@ -135,11 +135,11 @@ def tile_input_timestep_t_kernel(tc, t, W1, b1, W2, b2, out):
             w2g = ring.tile([P, 2, P, 4], BF16, name="w2g", tag="ring", align_bytes=64)
             w1gw = w1g[:].bitcast(F32)
             for a in range(2):
-                nc.vector.tensor_copy(
+                nc.scalar.copy(
                     out=w1gw[:, 2 * a : 2 * a + 2, :, :],
                     in_=wts[a][:].rearrange("p m u h -> p m h u"),
                 )
-            nc.vector.tensor_copy(
+            nc.scalar.copy(
                 out=w2g[:].bitcast(F32), in_=wts[2][:].rearrange("p m u h -> p m h u")
             )
             nc.vector.quantize_mx(
@@ -150,9 +150,6 @@ def tile_input_timestep_t_kernel(tc, t, W1, b1, W2, b2, out):
                 out=w2c[:].bitcast(FP8X4), scales=w2s[:],
                 in_=w2g[:].rearrange("p m h k -> p (m h k)"),
             )
-            nc.vector.tensor_copy(out=b1f[:], in_=b1raw[:].rearrange("p u e -> p (u e)"))
-            for j in range(2):
-                nc.vector.tensor_copy(out=b2f[:, j, :], in_=b2raw[:])
 
         def regroup(dst, src):
             nc.vector.tensor_copy(
@@ -184,13 +181,18 @@ def tile_input_timestep_t_kernel(tc, t, W1, b1, W2, b2, out):
             d = c - 1
             if d >= 0:
                 eg = egpool.tile([P, 4 * CB], BF16, name="eg", align_bytes=64)
-                for q in range(0, GT, GPIECE):
+                gt = GT if c < NCH else 0
+                for q in range(0, gt, GPIECE):
                     nc.gpsimd.tensor_scalar(
                         out=eg[:, 4 * q : 4 * (q + GPIECE)].rearrange("p (c k) -> p c k", k=4),
                         in0=eps[d][:, :, q : q + GPIECE].rearrange("p k c -> p c k"),
                         scalar1=1.0, scalar2=0.0, op0=ALU.mult, op1=ALU.add,
                     )
-                regroup(eg[:, 4 * GT :], eps[d][:, :, GT:])
+                if gt:
+                    regroup(eg[:, 4 * gt :], eps[d][:, :, gt:])
+                else:
+                    for s in range(2):
+                        regroup(eg[:, s * 4 * GB : (s + 1) * 4 * GB], eps[d][:, :, s * GB : (s + 1) * GB])
                 if d == WPREP_AFTER:
                     weight_prep()
                 for s in range(2):
@@ -220,6 +222,9 @@ def tile_input_timestep_t_kernel(tc, t, W1, b1, W2, b2, out):
                 out=hps[g][:, m, :], in_=ps1[:], func=ACT.Silu, bias=b1f[:, m : m + 1], scale=1.0
             )
 
+        nc.scalar.copy(out=b1f[:], in_=b1raw[:].rearrange("p u e -> p (u e)"))
+        for j in range(2):
+            nc.scalar.copy(out=b2f[:, j, :], in_=b2raw[:])
         for i in range(PRE):
             layer1_tile(i)
 

@@ -18,37 +18,55 @@ B, D, H, O = 8192, 512, 512, 256
 FLOPS = 2 * B * D * H + 2 * B * H * O
 
 CB = 1024
-NCH = B // CB
 GB = 512
 NG = B // GB
+NN = 16
+NPE = 7
+NSG = NG - NPE
+ST = NSG * GB
+NCH = (ST + CB - 1) // CB
+NBK = 4 * NPE
 FIRST = 256
 LADD = 2
 LSIL = 3
-WPREP_AFTER = 1
 GT = 768
-GPIECE = 768
-TBA = 4
-PRE = 40
-RATE = 2
+GTS = 384
+WT_AT = 2
+LA = 3
+SE = [0, 4, 4, 4, 3]
+VE = [0, 1, 1, 1, 1]
+NBE = 19
+LATE_EVERY = 3
+NSL = 4
+PRE = 20
+RATE = 3
 GH = 128
+AH0 = 2
+AH1 = 0
 
 
 def tile_input_timestep_t_kernel(tc, t, W1, b1, W2, b2, out):
     nc = tc.nc
     with ExitStack() as ctx:
         const = ctx.enter_context(tc.tile_pool(name="const", bufs=1))
-        ring = ctx.enter_context(tc.tile_pool(name="ring", bufs=20))
+        ring = ctx.enter_context(tc.tile_pool(name="ring", bufs=18))
         epool = ctx.enter_context(tc.tile_pool(name="epool", bufs=2))
         egpool = ctx.enter_context(tc.tile_pool(name="egpool", bufs=1))
+        pgpool = ctx.enter_context(tc.tile_pool(name="pgpool", bufs=3))
         hgpool = ctx.enter_context(tc.tile_pool(name="hgpool", bufs=2))
         cpool = ctx.enter_context(tc.tile_pool(name="cpool", bufs=6))
         zpool = ctx.enter_context(tc.tile_pool(name="zpool", bufs=4))
         psum = ctx.enter_context(tc.psum_pool(name="psum", bufs=8))
         ctx.enter_context(tc.manual_schedule())
 
-        pieces = [[(0, FIRST), (FIRST, CB)]] + [[(c * CB, (c + 1) * CB)] for c in range(1, NCH)]
+        CH = [(lo, min(lo + CB, ST)) for lo in range(0, ST, CB)]
+        pieces = [[(0, FIRST), (FIRST, CB)]] + [[CH[c]] for c in range(1, NCH)]
+        state = {"issued": 0, "next": 0, "mm1": 0}
 
-        tb = const.tile([P, B], BF16, name="tb")
+        def new_bank(shape, dtype):
+            return psum.tile(shape, dtype, name="bank", tag="bank")
+
+        tb = const.tile([P, ST], BF16, name="tb")
 
         def load_t(c):
             for lo, hi in pieces[c]:
@@ -62,94 +80,122 @@ def tile_input_timestep_t_kernel(tc, t, W1, b1, W2, b2, out):
         lo1, hi1 = pieces[0][1]
         nc.sync.dma_start(out=tb[:, lo1:hi1], in_=t[lo1:hi1].partition_broadcast(P))
         load_t(1)
-        w1raw = ring.tile([P, 4, D], BF16, name="w1raw", tag="ring", align_bytes=64)
-        nc.sync.dma_start(
-            out=w1raw[:].rearrange("p (u e) i -> p u e i", u=2),
-            in_=W1.rearrange("(u p e) i -> p u e i", u=2, e=2),
-        )
-        w2raw = ring.tile([P, 2, H], BF16, name="w2raw", tag="ring", align_bytes=64)
-        nc.sync.dma_start(out=w2raw[:], in_=W2.rearrange("(a p) h -> p a h", a=2))
-        for c in range(2, NCH):
-            load_t(c)
+        load_t(2)
         b1raw = const.tile([P, 2, 2], BF16, name="b1raw")
         b2raw = const.tile([P, O], BF16, name="b2raw")
         with nc.allow_non_contiguous_dma(reason="two small bias vectors, one value a partition"):
             nc.sync.dma_start(out=b1raw[:], in_=b1.rearrange("(u p e) -> p u e", u=2, e=2))
         nc.sync.dma_start(out=b2raw[:], in_=b2.partition_broadcast(P))
+        w1raw = const.tile([P, 4, D], BF16, name="w1raw")
+        nc.sync.dma_start(
+            out=w1raw[:].rearrange("p (u e) i -> p u e i", u=2),
+            in_=W1.rearrange("(u p e) i -> p u e i", u=2, e=2),
+        )
+        w2raw = const.tile([P, 2, H], BF16, name="w2raw")
+        nc.sync.dma_start(out=w2raw[:], in_=W2.rearrange("(a p) h -> p a h", a=2))
+        for c in range(3, NCH):
+            load_t(c)
 
         idx_i = const.tile([P, 4], I32, name="idx_i")
-        nc.gpsimd.iota(idx_i[:], pattern=[[256, 2], [1, 2]], base=0, channel_multiplier=2)
+        nc.gpsimd.iota(idx_i[:], pattern=[[1, 4]], base=0, channel_multiplier=4)
+        pid_i = const.tile([P, 1], I32, name="pid_i")
+        nc.gpsimd.iota(pid_i[:], pattern=[[1, 1]], base=0, channel_multiplier=1)
+        idx_f = const.tile([P, 8], F32, name="idx_f")
+        negphi = const.tile([P, 8], F32, name="negphi")
+        sbias = const.tile([P, 8], F32, name="sbias")
+        csin = const.tile([P, 8], F32, name="csin")
+        amp = const.tile([P, 8], F32, name="amp")
+
+        def angles(cols):
+            nc.vector.tensor_scalar_mul(out=negphi[:, cols], in0=idx_f[:, cols], scalar1=-math.pi / D)
+            nc.vector.tensor_scalar(
+                out=sbias[:, cols], in0=idx_f[:, cols], scalar1=math.pi / (2 * D), scalar2=math.pi / 4,
+                op0=ALU.mult, op1=ALU.add,
+            )
+
+        nc.vector.tensor_copy(out=idx_f[:, 0:4], in_=idx_i[:])
+        angles(slice(0, 4))
+        nc.scalar.activation(out=csin[:, 0:4], in_=sbias[:, 0:4], func=ACT.Sin)
+        jq_i = const.tile([P, 3], I32, name="jq_i")
+        nc.vector.tensor_single_scalar(out=jq_i[:, 0:1], in_=pid_i[:], scalar=NN - 1, op=ALU.bitwise_and)
+        nc.vector.tensor_single_scalar(out=jq_i[:, 1:2], in_=pid_i[:], scalar=4, op=ALU.logical_shift_right)
+        nc.vector.tensor_single_scalar(out=jq_i[:, 2:3], in_=pid_i[:], scalar=1, op=ALU.bitwise_and)
+        jq_f = const.tile([P, 3], F32, name="jq_f")
+        nc.vector.tensor_copy(out=jq_f[:], in_=jq_i[:])
+        argp = const.tile([P, 2], F32, name="argp")
+        for i in range(2):
+            nc.vector.tensor_scalar(
+                out=argp[:, i : i + 1], in0=jq_f[:, 0:1], scalar1=math.pi / NN,
+                scalar2=math.pi * (1 - NN) / (2 * NN) + i * math.pi / 2, op0=ALU.mult, op1=ALU.add,
+            )
+        sinp = const.tile([P, 2], F32, name="sinp")
+        nc.scalar.activation(out=sinp[:], in_=argp[:], func=ACT.Sin)
         ident = const.tile([P, P], F32, name="ident")
         make_identity(nc, ident[:])
-        idx_f = const.tile([P, 4], F32, name="idx_f")
-        nc.vector.tensor_copy(out=idx_f[:], in_=idx_i[:])
-        negphi = const.tile([P, 4], F32, name="negphi")
-        nc.vector.tensor_scalar_mul(out=negphi[:], in0=idx_f[:], scalar1=-math.pi / D)
-        sbias = const.tile([P, 4], F32, name="sbias")
-        nc.vector.tensor_scalar(
-            out=sbias[:], in0=idx_f[:], scalar1=math.pi / (2 * D), scalar2=math.pi / 4,
-            op0=ALU.mult, op1=ALU.add,
-        )
+        jf_i = const.tile([P, NN], I32, name="jf_i")
+        nc.gpsimd.iota(jf_i[:], pattern=[[1, NN]], base=0, channel_multiplier=0)
+        kf_i = const.tile([P, P], I32, name="kf_i")
+        nc.gpsimd.iota(kf_i[:], pattern=[[4, P]], base=-254, channel_multiplier=0)
+        qc_i = const.tile([P, P], I32, name="qc_i")
+        nc.gpsimd.iota(qc_i[:], pattern=[[1, P // NN], [0, NN]], base=NSG, channel_multiplier=0)
         identb = const.tile([P, P], BF16, name="identb")
         nc.vector.tensor_copy(out=identb[:], in_=ident[:])
-        csin = const.tile([P, 4], F32, name="csin")
-        nc.scalar.activation(out=csin[:], in_=sbias[:], func=ACT.Sin)
-        amp = const.tile([P, 4], F32, name="amp")
-        nc.vector.tensor_scalar_mul(out=amp[:], in0=csin[:], scalar1=2.0)
+        pid_f = const.tile([P, 1], F32, name="pid_f")
+        nc.vector.tensor_copy(out=pid_f[:], in_=pid_i[:])
+        sel = const.tile([P, P], BF16, name="sel")
+        nc.vector.tensor_scalar(out=sel[:], in0=qc_i[:], scalar1=pid_f[:, 0:1], scalar2=None, op0=ALU.is_equal)
 
-        tbps = {}
-
-        def broadcast_t(c):
-            tbp = psum.tile([P, CB], BF16, name="tbp", tag="bank")
-            tbps[c] = tbp
-            for s in range(2):
-                g = 2 * c + s
-                nc.tensor.matmul(
-                    out=tbp[:, s * GB : (s + 1) * GB],
-                    lhsT=identb[:, g : g + 1].to_broadcast([P, P]),
-                    rhs=t16[:], start=True, stop=True,
-                )
-
-        for c in range(TBA):
-            broadcast_t(c)
-
+        ec = const.tile([P, B], U32, name="ec", align_bytes=64)
+        es = const.tile([P, B], U8, name="es", align_bytes=64)
         w1c = const.tile([P, H], U32, name="w1c", align_bytes=64)
         w1s = const.tile([P, H], U8, name="w1s", align_bytes=64)
         w2c = const.tile([P, O], U32, name="w2c", align_bytes=64)
         w2s = const.tile([P, O], U8, name="w2s", align_bytes=64)
         b1f = const.tile([P, 4], F32, name="b1f")
-        b2f = const.tile([P, 2, O], F32, name="b2f")
-        wts = []
-        for a in range(3):
-            wt = psum.tile([P, 2, 2, P], F32, name="wt", tag="bank")
-            for m in range(2):
-                src = w1raw[:, 2 * a + m, :] if a < 2 else w2raw[:, m, :]
-                for u in range(2):
-                    nc.tensor.transpose(
-                        wt[:, m, u, :], src.bitcast(F32)[:, u * P : (u + 1) * P], ident[:]
-                    )
-            wts.append(wt)
+        b2f = const.tile([P, O], F32, name="b2f")
+        feat = const.tile([P, 4, GB], F32, name="feat")
+        aall = const.tile([P, NPE, P], F32, name="aall")
+        rs = const.tile([P, 1], F32, name="rs")
+        banks, pgs, pending, ready = {}, {}, [], set()
 
-        def weight_prep():
-            w1g = ring.tile([P, 4, P, 4], BF16, name="w1g", tag="ring", align_bytes=64)
-            w2g = ring.tile([P, 2, P, 4], BF16, name="w2g", tag="ring", align_bytes=64)
-            w1gw = w1g[:].bitcast(F32)
-            for a in range(2):
-                nc.scalar.copy(
-                    out=w1gw[:, 2 * a : 2 * a + 2, :, :],
-                    in_=wts[a][:].rearrange("p m u h -> p m h u"),
+        def issue_to(n):
+            for b in range(state["issued"], min(n, NBK)):
+                q, r = divmod(b, 4)
+                banks[b] = new_bank([P, GB], F32)
+                nc.tensor.matmul(
+                    out=banks[b][:].rearrange("p (k c) -> p k c", k=4),
+                    lhsT=aall[:, q, :],
+                    rhs=feat[:, :, r * P : (r + 1) * P],
+                    start=True, stop=True,
                 )
-            nc.scalar.copy(
-                out=w2g[:].bitcast(F32), in_=wts[2][:].rearrange("p m u h -> p m h u")
-            )
-            nc.vector.quantize_mx(
-                out=w1c[:].bitcast(FP8X4), scales=w1s[:],
-                in_=w1g[:].rearrange("p m h k -> p (m h k)"),
-            )
-            nc.vector.quantize_mx(
-                out=w2c[:].bitcast(FP8X4), scales=w2s[:],
-                in_=w2g[:].rearrange("p m h k -> p (m h k)"),
-            )
+                state["issued"] = b + 1
+
+        def empty_banks(n, on_scalar):
+            for i in range(n):
+                b = state["next"]
+                if b >= NBK:
+                    return
+                issue_to(b + 1)
+                state["next"] = b + 1
+                q, r = divmod(b, 4)
+                if r == 0:
+                    pgs[q] = pgpool.tile([P, 4 * GB], BF16, name="pg", align_bytes=64)
+                dst = pgs[q][:, r * GB : (r + 1) * GB].rearrange("p (c k) -> p c k", k=4)
+                src = banks[b][:].rearrange("p (k c) -> p c k", k=4)
+                if on_scalar:
+                    nc.scalar.activation(out=dst, in_=src, func=ACT.Copy, scale=rs[:, 0:1])
+                else:
+                    nc.vector.tensor_scalar_mul(out=dst, in0=src, scalar1=rs[:, 0:1])
+                if r == 3:
+                    pending.append(q)
+                issue_to(min(b + 1 + LA, max(NBE, b + 1)))
+
+        def quantise_pending():
+            for q in pending:
+                cols = slice((NSG + q) * GB, (NSG + q + 1) * GB)
+                nc.vector.quantize_mx(out=ec[:, cols].bitcast(FP8X4), scales=es[:, cols], in_=pgs[q][:])
+                ready.add(NSG + q)
+            pending.clear()
 
         def regroup(dst, src):
             nc.vector.tensor_copy(
@@ -157,11 +203,117 @@ def tile_input_timestep_t_kernel(tc, t, W1, b1, W2, b2, out):
                 in_=src.rearrange("p k (c i) -> p c k i", i=4),
             )
 
-        ec = const.tile([P, B], U32, name="ec", align_bytes=64)
-        es = const.tile([P, B], U8, name="es", align_bytes=64)
+        tbps = {}
+
+        def broadcast_t(c):
+            tbp = new_bank([P, CB], BF16)
+            tbps[c] = tbp
+            for s in range((CH[c][1] - CH[c][0]) // GB):
+                g = 2 * c + s
+                nc.tensor.matmul(
+                    out=tbp[:, s * GB : (s + 1) * GB],
+                    lhsT=identb[:, g : g + 1].to_broadcast([P, P]),
+                    rhs=t16[:], start=True, stop=True,
+                )
+
+        broadcast_t(0)
+        t8 = new_bank([P, GB], BF16)
+        nc.tensor.matmul(out=t8[:], lhsT=sel[:], rhs=t16[:], start=True, stop=True)
+        broadcast_t(1)
+        sgn = const.tile([P, 1], F32, name="sgn")
+        nc.vector.tensor_scalar(
+            out=sgn[:], in0=jq_f[:, 2:3], scalar1=-2.0, scalar2=1.0, op0=ALU.mult, op1=ALU.add
+        )
+        jf_f = const.tile([P, NN], F32, name="jf_f")
+        nc.vector.tensor_copy(out=jf_f[:], in_=jf_i[:])
+        ones = const.tile([P, 2], F32, name="ones")
+        nc.vector.memset(ones[:], 1.0)
+        nc.vector.tensor_scalar_mul(out=amp[:, 0:4], in0=csin[:, 0:4], scalar1=2.0)
+        kap0 = const.tile([P, 1], F32, name="kap0")
+        nc.vector.tensor_scalar(
+            out=kap0[:], in0=sinp[:, 0:1], scalar1=256.0, scalar2=254.0, op0=ALU.mult, op1=ALU.add
+        )
+        nc.vector.tensor_scalar_add(out=idx_f[:, 4:8], in0=jf_f[:, 0:4], scalar1=kap0[:, 0:1])
+        angles(slice(4, 8))
+        nc.scalar.activation(out=csin[:, 4:8], in_=sbias[:, 4:8], func=ACT.Sin)
+        wp = const.tile([P, 1], F32, name="wp")
+        nc.vector.tensor_mul(out=wp[:], in0=sinp[:, 1:2], in1=sgn[:])
+        wq = const.tile([P, 8], F32, name="wq")
+        nc.vector.tensor_scalar(
+            out=wq[:], in0=jf_f[:, 0:8], scalar1=jq_f[:, 1:2], scalar2=wp[:, 0:1],
+            op0=ALU.is_equal, op1=ALU.mult,
+        )
+        dm = const.tile([P, P], F32, name="dm")
+        nc.vector.tensor_scalar(
+            out=dm[:], in0=kf_i[:], scalar1=1.0 / 256, scalar2=sinp[:, 0:1], op0=ALU.mult, op1=ALU.subtract
+        )
+        rm = const.tile([P, P], F32, name="rm")
+        nc.vector.reciprocal(out=rm[:], in_=dm[:])
+        nc.vector.tensor_scalar_mul(out=amp[:, 4:8], in0=csin[:, 4:8], scalar1=2.0)
+        nc.vector.tensor_tensor(
+            out=aall[:], in0=rm[:].unsqueeze(1).to_broadcast([P, NPE, P]),
+            in1=wq[:, 0:NPE].unsqueeze(2).to_broadcast([P, NPE, P]), op=ALU.mult,
+        )
+        nrm = new_bank([P, GB], F32)
+        nc.tensor.matmul(out=nrm[:, 0:2], lhsT=aall[:, 0, :], rhs=ones[:], start=True, stop=True)
+
+        def features():
+            sns = []
+            for k in range(4):
+                sn = ring.tile([P, CB], F32, name="sn", tag="ring", align_bytes=64)
+                sns.append(sn)
+                nc.scalar.activation(
+                    out=sn[:, 0:GB], in_=t8[:], func=ACT.Sin,
+                    bias=sbias[:, 4 + k : 5 + k], scale=negphi[:, 4 + k : 5 + k],
+                )
+            for k in range(4):
+                nc.vector.scalar_tensor_tensor(
+                    out=feat[:, k, :], in0=sns[k][:, 0:GB], scalar=amp[:, 4 + k : 5 + k], in1=t8[:],
+                    op0=ALU.mult, op1=ALU.mult,
+                )
+            nc.vector.reciprocal(out=rs[:], in_=nrm[:, 0:1])
+            issue_to(LA)
+            nc.vector.tensor_copy(out=b1f[:], in_=b1raw[:].rearrange("p u e -> p (u e)"))
+            nc.vector.tensor_copy(out=b2f[:], in_=b2raw[:])
+
+        wts, wgs = [], {}
+
+        def weight_transposes():
+            for a in range(3):
+                wt = new_bank([P, 2, 2, P], F32)
+                for m in range(2):
+                    for u in range(2):
+                        if a < 2:
+                            src = w1raw[:, 2 * a + m, :].bitcast(F32)[:, u : 2 * P : 2]
+                        else:
+                            src = w2raw[:, m, :].bitcast(F32)[:, u * P : (u + 1) * P]
+                        nc.tensor.transpose(wt[:, m, u, :], src, ident[:])
+                wts.append(wt)
+
+        def weight_copy(a):
+            if a == 0:
+                wgs[1] = ring.tile([P, 4, P, 4], BF16, name="w1g", tag="ring", align_bytes=64)
+            if a == 2:
+                wgs[2] = ring.tile([P, 2, P, 4], BF16, name="w2g", tag="ring", align_bytes=64)
+                dst = wgs[2][:].bitcast(F32)
+            else:
+                dst = wgs[1][:].bitcast(F32)[:, 2 * a : 2 * a + 2, :, :]
+            nc.scalar.copy(out=dst, in_=wts[a][:].rearrange("p m u h -> p m h u"))
+
+        def weight_quantise():
+            nc.vector.quantize_mx(
+                out=w1c[:].bitcast(FP8X4), scales=w1s[:], in_=wgs[1][:].rearrange("p m h k -> p (m h k)")
+            )
+            nc.vector.quantize_mx(
+                out=w2c[:].bitcast(FP8X4), scales=w2s[:], in_=wgs[2][:].rearrange("p m h k -> p (m h k)")
+            )
+
         eps = {}
         for c in range(NCH + 1):
             if c < NCH:
+                if c == WT_AT:
+                    weight_transposes()
+                base = CH[c][0]
                 ep = epool.tile([P, 4, CB], BF16, name="ep")
                 eps[c] = ep
                 for lo, hi in pieces[c]:
@@ -172,67 +324,90 @@ def tile_input_timestep_t_kernel(tc, t, W1, b1, W2, b2, out):
                             bias=sbias[:, m : m + 1], scale=negphi[:, m : m + 1],
                         )
                         nc.vector.scalar_tensor_tensor(
-                            out=ep[:, m, lo - c * CB : hi - c * CB], in0=sn[:, 0 : hi - lo],
-                            scalar=amp[:, m : m + 1], in1=tbps[c][:, lo - c * CB : hi - c * CB],
+                            out=ep[:, m, lo - base : hi - base], in0=sn[:, 0 : hi - lo],
+                            scalar=amp[:, m : m + 1], in1=tbps[c][:, lo - base : hi - base],
                             op0=ALU.mult, op1=ALU.mult,
                         )
-                if c + TBA < NCH:
-                    broadcast_t(c + TBA)
+                        if c == 0 and lo == 0 and m == 3:
+                            features()
+                        if hi == CH[c][1] and m >= 4 - SE[c]:
+                            empty_banks(1, True)
+                        if c == WT_AT and m >= 1:
+                            weight_copy(m - 1)
+                        if c >= 1 and m == 1 and c + 1 < NCH:
+                            broadcast_t(c + 1)
+                empty_banks(VE[c], False)
+
             d = c - 1
             if d >= 0:
+                wd = CH[d][1] - CH[d][0]
                 eg = egpool.tile([P, 4 * CB], BF16, name="eg", align_bytes=64)
-                gt = GT if c < NCH else 0
-                for q in range(0, gt, GPIECE):
+                gt = 0
+                if c < NCH:
+                    gt = GT if CH[c][1] - CH[c][0] == CB else GTS
+                if gt:
                     nc.gpsimd.tensor_scalar(
-                        out=eg[:, 4 * q : 4 * (q + GPIECE)].rearrange("p (c k) -> p c k", k=4),
-                        in0=eps[d][:, :, q : q + GPIECE].rearrange("p k c -> p c k"),
+                        out=eg[:, 0 : 4 * gt].rearrange("p (c k) -> p c k", k=4),
+                        in0=eps[d][:, :, 0:gt].rearrange("p k c -> p c k"),
                         scalar1=1.0, scalar2=0.0, op0=ALU.mult, op1=ALU.add,
                     )
-                if gt:
-                    regroup(eg[:, 4 * gt :], eps[d][:, :, gt:])
-                else:
-                    for s in range(2):
-                        regroup(eg[:, s * 4 * GB : (s + 1) * 4 * GB], eps[d][:, :, s * GB : (s + 1) * GB])
-                if d == WPREP_AFTER:
-                    weight_prep()
-                for s in range(2):
-                    half = slice(d * CB + s * GB, d * CB + (s + 1) * GB)
+                regroup(eg[:, 4 * gt : 4 * wd], eps[d][:, :, gt:wd])
+                quantise_pending()
+                if d == WT_AT:
+                    weight_quantise()
+                for s in range(wd // GB):
+                    half = slice(CH[d][0] + s * GB, CH[d][0] + (s + 1) * GB)
                     nc.vector.quantize_mx(
                         out=ec[:, half].bitcast(FP8X4), scales=es[:, half],
                         in_=eg[:, s * 4 * GB : (s + 1) * 4 * GB],
                     )
+                    ready.add(CH[d][0] // GB + s)
 
         hps = {}
 
-        def layer1_tile(i):
+        ps1s = {}
+
+        def layer1_matmuls(n):
+            for i in range(state["mm1"], min(n, 4 * NG)):
+                g, m = divmod(i, 4)
+                if g not in ready:
+                    return
+                cols = slice(g * GB, (g + 1) * GB)
+                ps1s[i] = new_bank([P, GB], F32)
+                nc.tensor.matmul_mx(
+                    out=ps1s[i][:],
+                    lhsT=w1c[:, m * P : (m + 1) * P].bitcast(FP8X4),
+                    lhsT_scale=w1s[:, m * P : (m + 1) * P],
+                    rhs=ec[:, cols].bitcast(FP8X4),
+                    rhs_scale=es[:, cols],
+                    start=True, stop=True,
+                )
+                state["mm1"] = i + 1
+
+        def layer1_tile(i, ahead):
             g, m = divmod(i, 4)
-            cols = slice(g * GB, (g + 1) * GB)
+            layer1_matmuls(i + 1 + ahead)
+            assert i < state["mm1"]
             if m == 0:
                 hps[g] = ring.tile([P, 4, GB], BF16, name="hp", tag="ring", align_bytes=64)
-            ps1 = psum.tile([P, GB], F32, name="ps1", tag="bank")
-            nc.tensor.matmul_mx(
-                out=ps1[:],
-                lhsT=w1c[:, m * P : (m + 1) * P].bitcast(FP8X4),
-                lhsT_scale=w1s[:, m * P : (m + 1) * P],
-                rhs=ec[:, cols].bitcast(FP8X4),
-                rhs_scale=es[:, cols],
-                start=True, stop=True,
-            )
             nc.scalar.activation(
-                out=hps[g][:, m, :], in_=ps1[:], func=ACT.Silu, bias=b1f[:, m : m + 1], scale=1.0
+                out=hps[g][:, m, :], in_=ps1s[i][:], func=ACT.Silu, bias=b1f[:, m : m + 1], scale=1.0
             )
 
-        nc.scalar.copy(out=b1f[:], in_=b1raw[:].rearrange("p u e -> p (u e)"))
-        for j in range(2):
-            nc.scalar.copy(out=b2f[:, j, :], in_=b2raw[:])
         for i in range(PRE):
-            layer1_tile(i)
+            layer1_tile(i, AH0)
+            if i % LATE_EVERY == 1:
+                if state["issued"] > state["next"] and state["next"] < NBE + NSL:
+                    empty_banks(1, True)
+                if state["issued"] < NBE + NSL + 1:
+                    issue_to(state["issued"] + 1)
 
         out_v = out.rearrange("(g a p) o -> g p a o", a=4, p=P)
         hgs, hcs, hss, ps2s, zs = {}, {}, {}, {}, {}
         for k in range(NG + LSIL + 1):
+            made = state["issued"]
             for i in range(PRE + RATE * k, min(PRE + RATE * (k + 1), 4 * NG)):
-                layer1_tile(i)
+                layer1_tile(i, AH1)
             if k < NG:
                 if k in hgs:
                     regroup(hgs[k][:, 4 * GH :], hps[k][:, :, GH:])
@@ -245,7 +420,7 @@ def tile_input_timestep_t_kernel(tc, t, W1, b1, W2, b2, out):
                 hss[g] = cpool.tile([P, GB], U8, name="hs", align_bytes=64)
                 nc.vector.quantize_mx(out=hcs[g][:].bitcast(FP8X4), scales=hss[g][:], in_=hgs[g][:])
                 for s in range(2):
-                    ps2 = psum.tile([P, 2, O], F32, name="ps2", tag="bank")
+                    ps2 = new_bank([P, 2, O], F32)
                     ps2s[g, s] = ps2
                     for j in range(2):
                         bt = 2 * s + j
@@ -257,6 +432,7 @@ def tile_input_timestep_t_kernel(tc, t, W1, b1, W2, b2, out):
                             rhs_scale=w2s[:],
                             start=True, stop=True,
                         )
+            issue_to(state["issued"] + 1)
             ga = k - LADD
             if 0 <= ga < NG and k + 1 < NG:
                 hgs[k + 1] = hgpool.tile([P, 4 * GB], BF16, name="hg", align_bytes=64)
@@ -269,8 +445,12 @@ def tile_input_timestep_t_kernel(tc, t, W1, b1, W2, b2, out):
                 zs[ga] = zpool.tile([P, 4, O], F32, name="z")
                 for s in range(2):
                     nc.vector.tensor_tensor(
-                        out=zs[ga][:, 2 * s : 2 * s + 2, :], in0=ps2s[ga, s][:], in1=b2f[:], op=ALU.add
+                        out=zs[ga][:, 2 * s : 2 * s + 2, :], in0=ps2s[ga, s][:],
+                        in1=b2f[:].unsqueeze(1).to_broadcast([P, 2, O]), op=ALU.add
                     )
+            if state["next"] < made:
+                empty_banks(1, False)
+            quantise_pending()
             gs = k - LSIL
             if 0 <= gs < NG:
                 parts = 2 if gs == NG - 1 else 1

import math
from contextlib import ExitStack

import concourse.mybir as mybir
from concourse.masks import make_identity

F32 = mybir.dt.float32
BF16 = mybir.dt.bfloat16
I32 = mybir.dt.int32
U32 = mybir.dt.uint32
U8 = mybir.dt.uint8
FP8X4 = mybir.dt.float8_e4m3fn_x4
ACT = mybir.ActivationFunctionType
ALU = mybir.AluOpType

P = 128
B, D, H, O = 8192, 512, 512, 256
FLOPS = 2 * B * D * H + 2 * B * H * O

CB = 1024
GB = 512
NG = B // GB
NN = 16
NPE = 7
NSG = NG - NPE
ST = NSG * GB
NCH = (ST + CB - 1) // CB
NBK = 4 * NPE
FIRST = 256
LADD = 2
LSIL = 3
GT = 768
GTS = 384
WT_AT = 2
LA = 3
SE = [0, 4, 4, 4, 3]
VE = [0, 1, 1, 1, 1]
NBE = 19
LATE_EVERY = 3
NSL = 4
PRE = 20
RATE = 3
GH = 128
AH0 = 2
AH1 = 0


def tile_input_timestep_t_kernel(tc, t, W1, b1, W2, b2, out):
    nc = tc.nc
    with ExitStack() as ctx:
        const = ctx.enter_context(tc.tile_pool(name="const", bufs=1))
        ring = ctx.enter_context(tc.tile_pool(name="ring", bufs=18))
        epool = ctx.enter_context(tc.tile_pool(name="epool", bufs=2))
        egpool = ctx.enter_context(tc.tile_pool(name="egpool", bufs=1))
        pgpool = ctx.enter_context(tc.tile_pool(name="pgpool", bufs=3))
        hgpool = ctx.enter_context(tc.tile_pool(name="hgpool", bufs=2))
        cpool = ctx.enter_context(tc.tile_pool(name="cpool", bufs=6))
        zpool = ctx.enter_context(tc.tile_pool(name="zpool", bufs=4))
        psum = ctx.enter_context(tc.psum_pool(name="psum", bufs=8))
        ctx.enter_context(tc.manual_schedule())

        CH = [(lo, min(lo + CB, ST)) for lo in range(0, ST, CB)]
        pieces = [[(0, FIRST), (FIRST, CB)]] + [[CH[c]] for c in range(1, NCH)]
        state = {"issued": 0, "next": 0, "mm1": 0}

        def new_bank(shape, dtype):
            return psum.tile(shape, dtype, name="bank", tag="bank")

        tb = const.tile([P, ST], BF16, name="tb")

        def load_t(c):
            for lo, hi in pieces[c]:
                nc.sync.dma_start(out=tb[:, lo:hi], in_=t[lo:hi].partition_broadcast(P))

        t16 = const.tile([P, GB], BF16, name="t16")
        nc.vector.memset(t16[:], 0.0)
        lo0, hi0 = pieces[0][0]
        nc.sync.dma_start(out=tb[:, lo0:hi0], in_=t[lo0:hi0].partition_broadcast(P))
        nc.sync.dma_start(out=t16[0:NG, :], in_=t.rearrange("(g n) -> g n", n=GB))
        lo1, hi1 = pieces[0][1]
        nc.sync.dma_start(out=tb[:, lo1:hi1], in_=t[lo1:hi1].partition_broadcast(P))
        load_t(1)
        load_t(2)
        b1raw = const.tile([P, 2, 2], BF16, name="b1raw")
        b2raw = const.tile([P, O], BF16, name="b2raw")
        with nc.allow_non_contiguous_dma(reason="two small bias vectors, one value a partition"):
            nc.sync.dma_start(out=b1raw[:], in_=b1.rearrange("(u p e) -> p u e", u=2, e=2))
        nc.sync.dma_start(out=b2raw[:], in_=b2.partition_broadcast(P))
        w1raw = const.tile([P, 4, D], BF16, name="w1raw")
        nc.sync.dma_start(
            out=w1raw[:].rearrange("p (u e) i -> p u e i", u=2),
            in_=W1.rearrange("(u p e) i -> p u e i", u=2, e=2),
        )
        w2raw = const.tile([P, 2, H], BF16, name="w2raw")
        nc.sync.dma_start(out=w2raw[:], in_=W2.rearrange("(a p) h -> p a h", a=2))
        for c in range(3, NCH):
            load_t(c)

        idx_i = const.tile([P, 4], I32, name="idx_i")
        nc.gpsimd.iota(idx_i[:], pattern=[[1, 4]], base=0, channel_multiplier=4)
        pid_i = const.tile([P, 1], I32, name="pid_i")
        nc.gpsimd.iota(pid_i[:], pattern=[[1, 1]], base=0, channel_multiplier=1)
        idx_f = const.tile([P, 8], F32, name="idx_f")
        negphi = const.tile([P, 8], F32, name="negphi")
        sbias = const.tile([P, 8], F32, name="sbias")
        csin = const.tile([P, 8], F32, name="csin")
        amp = const.tile([P, 8], F32, name="amp")

        def angles(cols):
            nc.vector.tensor_scalar_mul(out=negphi[:, cols], in0=idx_f[:, cols], scalar1=-math.pi / D)
            nc.vector.tensor_scalar(
                out=sbias[:, cols], in0=idx_f[:, cols], scalar1=math.pi / (2 * D), scalar2=math.pi / 4,
                op0=ALU.mult, op1=ALU.add,
            )

        nc.vector.tensor_copy(out=idx_f[:, 0:4], in_=idx_i[:])
        angles(slice(0, 4))
        nc.scalar.activation(out=csin[:, 0:4], in_=sbias[:, 0:4], func=ACT.Sin)
        jq_i = const.tile([P, 3], I32, name="jq_i")
        nc.vector.tensor_single_scalar(out=jq_i[:, 0:1], in_=pid_i[:], scalar=NN - 1, op=ALU.bitwise_and)
        nc.vector.tensor_single_scalar(out=jq_i[:, 1:2], in_=pid_i[:], scalar=4, op=ALU.logical_shift_right)
        nc.vector.tensor_single_scalar(out=jq_i[:, 2:3], in_=pid_i[:], scalar=1, op=ALU.bitwise_and)
        jq_f = const.tile([P, 3], F32, name="jq_f")
        nc.vector.tensor_copy(out=jq_f[:], in_=jq_i[:])
        argp = const.tile([P, 2], F32, name="argp")
        for i in range(2):
            nc.vector.tensor_scalar(
                out=argp[:, i : i + 1], in0=jq_f[:, 0:1], scalar1=math.pi / NN,
                scalar2=math.pi * (1 - NN) / (2 * NN) + i * math.pi / 2, op0=ALU.mult, op1=ALU.add,
            )
        sinp = const.tile([P, 2], F32, name="sinp")
        nc.scalar.activation(out=sinp[:], in_=argp[:], func=ACT.Sin)
        ident = const.tile([P, P], F32, name="ident")
        make_identity(nc, ident[:])
        jf_i = const.tile([P, NN], I32, name="jf_i")
        nc.gpsimd.iota(jf_i[:], pattern=[[1, NN]], base=0, channel_multiplier=0)
        kf_i = const.tile([P, P], I32, name="kf_i")
        nc.gpsimd.iota(kf_i[:], pattern=[[4, P]], base=-254, channel_multiplier=0)
        qc_i = const.tile([P, P], I32, name="qc_i")
        nc.gpsimd.iota(qc_i[:], pattern=[[1, P // NN], [0, NN]], base=NSG, channel_multiplier=0)
        identb = const.tile([P, P], BF16, name="identb")
        nc.vector.tensor_copy(out=identb[:], in_=ident[:])
        pid_f = const.tile([P, 1], F32, name="pid_f")
        nc.vector.tensor_copy(out=pid_f[:], in_=pid_i[:])
        sel = const.tile([P, P], BF16, name="sel")
        nc.vector.tensor_scalar(out=sel[:], in0=qc_i[:], scalar1=pid_f[:, 0:1], scalar2=None, op0=ALU.is_equal)

        ec = const.tile([P, B], U32, name="ec", align_bytes=64)
        es = const.tile([P, B], U8, name="es", align_bytes=64)
        w1c = const.tile([P, H], U32, name="w1c", align_bytes=64)
        w1s = const.tile([P, H], U8, name="w1s", align_bytes=64)
        w2c = const.tile([P, O], U32, name="w2c", align_bytes=64)
        w2s = const.tile([P, O], U8, name="w2s", align_bytes=64)
        b1f = const.tile([P, 4], F32, name="b1f")
        b2f = const.tile([P, O], F32, name="b2f")
        feat = const.tile([P, 4, GB], F32, name="feat")
        aall = const.tile([P, NPE, P], F32, name="aall")
        rs = const.tile([P, 1], F32, name="rs")
        banks, pgs, pending, ready = {}, {}, [], set()

        def issue_to(n):
            for b in range(state["issued"], min(n, NBK)):
                q, r = divmod(b, 4)
                banks[b] = new_bank([P, GB], F32)
                nc.tensor.matmul(
                    out=banks[b][:].rearrange("p (k c) -> p k c", k=4),
                    lhsT=aall[:, q, :],
                    rhs=feat[:, :, r * P : (r + 1) * P],
                    start=True, stop=True,
                )
                state["issued"] = b + 1

        def empty_banks(n, on_scalar):
            for i in range(n):
                b = state["next"]
                if b >= NBK:
                    return
                issue_to(b + 1)
                state["next"] = b + 1
                q, r = divmod(b, 4)
                if r == 0:
                    pgs[q] = pgpool.tile([P, 4 * GB], BF16, name="pg", align_bytes=64)
                dst = pgs[q][:, r * GB : (r + 1) * GB].rearrange("p (c k) -> p c k", k=4)
                src = banks[b][:].rearrange("p (k c) -> p c k", k=4)
                if on_scalar:
                    nc.scalar.activation(out=dst, in_=src, func=ACT.Copy, scale=rs[:, 0:1])
                else:
                    nc.vector.tensor_scalar_mul(out=dst, in0=src, scalar1=rs[:, 0:1])
                if r == 3:
                    pending.append(q)
                issue_to(min(b + 1 + LA, max(NBE, b + 1)))

        def quantise_pending():
            for q in pending:
                cols = slice((NSG + q) * GB, (NSG + q + 1) * GB)
                nc.vector.quantize_mx(out=ec[:, cols].bitcast(FP8X4), scales=es[:, cols], in_=pgs[q][:])
                ready.add(NSG + q)
            pending.clear()

        def regroup(dst, src):
            nc.vector.tensor_copy(
                out=dst.rearrange("p (c i k) -> p c k i", i=4, k=4),
                in_=src.rearrange("p k (c i) -> p c k i", i=4),
            )

        tbps = {}

        def broadcast_t(c):
            tbp = new_bank([P, CB], BF16)
            tbps[c] = tbp
            for s in range((CH[c][1] - CH[c][0]) // GB):
                g = 2 * c + s
                nc.tensor.matmul(
                    out=tbp[:, s * GB : (s + 1) * GB],
                    lhsT=identb[:, g : g + 1].to_broadcast([P, P]),
                    rhs=t16[:], start=True, stop=True,
                )

        broadcast_t(0)
        t8 = new_bank([P, GB], BF16)
        nc.tensor.matmul(out=t8[:], lhsT=sel[:], rhs=t16[:], start=True, stop=True)
        broadcast_t(1)
        sgn = const.tile([P, 1], F32, name="sgn")
        nc.vector.tensor_scalar(
            out=sgn[:], in0=jq_f[:, 2:3], scalar1=-2.0, scalar2=1.0, op0=ALU.mult, op1=ALU.add
        )
        jf_f = const.tile([P, NN], F32, name="jf_f")
        nc.vector.tensor_copy(out=jf_f[:], in_=jf_i[:])
        ones = const.tile([P, 2], F32, name="ones")
        nc.vector.memset(ones[:], 1.0)
        nc.vector.tensor_scalar_mul(out=amp[:, 0:4], in0=csin[:, 0:4], scalar1=2.0)
        kap0 = const.tile([P, 1], F32, name="kap0")
        nc.vector.tensor_scalar(
            out=kap0[:], in0=sinp[:, 0:1], scalar1=256.0, scalar2=254.0, op0=ALU.mult, op1=ALU.add
        )
        nc.vector.tensor_scalar_add(out=idx_f[:, 4:8], in0=jf_f[:, 0:4], scalar1=kap0[:, 0:1])
        angles(slice(4, 8))
        nc.scalar.activation(out=csin[:, 4:8], in_=sbias[:, 4:8], func=ACT.Sin)
        wp = const.tile([P, 1], F32, name="wp")
        nc.vector.tensor_mul(out=wp[:], in0=sinp[:, 1:2], in1=sgn[:])
        wq = const.tile([P, 8], F32, name="wq")
        nc.vector.tensor_scalar(
            out=wq[:], in0=jf_f[:, 0:8], scalar1=jq_f[:, 1:2], scalar2=wp[:, 0:1],
            op0=ALU.is_equal, op1=ALU.mult,
        )
        dm = const.tile([P, P], F32, name="dm")
        nc.vector.tensor_scalar(
            out=dm[:], in0=kf_i[:], scalar1=1.0 / 256, scalar2=sinp[:, 0:1], op0=ALU.mult, op1=ALU.subtract
        )
        rm = const.tile([P, P], F32, name="rm")
        nc.vector.reciprocal(out=rm[:], in_=dm[:])
        nc.vector.tensor_scalar_mul(out=amp[:, 4:8], in0=csin[:, 4:8], scalar1=2.0)
        nc.vector.tensor_tensor(
            out=aall[:], in0=rm[:].unsqueeze(1).to_broadcast([P, NPE, P]),
            in1=wq[:, 0:NPE].unsqueeze(2).to_broadcast([P, NPE, P]), op=ALU.mult,
        )
        nrm = new_bank([P, GB], F32)
        nc.tensor.matmul(out=nrm[:, 0:2], lhsT=aall[:, 0, :], rhs=ones[:], start=True, stop=True)

        def features():
            sns = []
            for k in range(4):
                sn = ring.tile([P, CB], F32, name="sn", tag="ring", align_bytes=64)
                sns.append(sn)
                nc.scalar.activation(
                    out=sn[:, 0:GB], in_=t8[:], func=ACT.Sin,
                    bias=sbias[:, 4 + k : 5 + k], scale=negphi[:, 4 + k : 5 + k],
                )
            for k in range(4):
                nc.vector.scalar_tensor_tensor(
                    out=feat[:, k, :], in0=sns[k][:, 0:GB], scalar=amp[:, 4 + k : 5 + k], in1=t8[:],
                    op0=ALU.mult, op1=ALU.mult,
                )
            nc.vector.reciprocal(out=rs[:], in_=nrm[:, 0:1])
            issue_to(LA)
            nc.vector.tensor_copy(out=b1f[:], in_=b1raw[:].rearrange("p u e -> p (u e)"))
            nc.vector.tensor_copy(out=b2f[:], in_=b2raw[:])

        wts, wgs = [], {}

        def weight_transposes():
            for a in range(3):
                wt = new_bank([P, 2, 2, P], F32)
                for m in range(2):
                    for u in range(2):
                        if a < 2:
                            src = w1raw[:, 2 * a + m, :].bitcast(F32)[:, u : 2 * P : 2]
                        else:
                            src = w2raw[:, m, :].bitcast(F32)[:, u * P : (u + 1) * P]
                        nc.tensor.transpose(wt[:, m, u, :], src, ident[:])
                wts.append(wt)

        def weight_copy(a):
            if a == 0:
                wgs[1] = ring.tile([P, 4, P, 4], BF16, name="w1g", tag="ring", align_bytes=64)
            if a == 2:
                wgs[2] = ring.tile([P, 2, P, 4], BF16, name="w2g", tag="ring", align_bytes=64)
                dst = wgs[2][:].bitcast(F32)
            else:
                dst = wgs[1][:].bitcast(F32)[:, 2 * a : 2 * a + 2, :, :]
            nc.scalar.copy(out=dst, in_=wts[a][:].rearrange("p m u h -> p m h u"))

        def weight_quantise():
            nc.vector.quantize_mx(
                out=w1c[:].bitcast(FP8X4), scales=w1s[:], in_=wgs[1][:].rearrange("p m h k -> p (m h k)")
            )
            nc.vector.quantize_mx(
                out=w2c[:].bitcast(FP8X4), scales=w2s[:], in_=wgs[2][:].rearrange("p m h k -> p (m h k)")
            )

        eps = {}
        for c in range(NCH + 1):
            if c < NCH:
                if c == WT_AT:
                    weight_transposes()
                base = CH[c][0]
                ep = epool.tile([P, 4, CB], BF16, name="ep")
                eps[c] = ep
                for lo, hi in pieces[c]:
                    for m in range(4):
                        sn = ring.tile([P, CB], F32, name="sn", tag="ring", align_bytes=64)
                        nc.scalar.activation(
                            out=sn[:, 0 : hi - lo], in_=tb[:, lo:hi], func=ACT.Sin,
                            bias=sbias[:, m : m + 1], scale=negphi[:, m : m + 1],
                        )
                        nc.vector.scalar_tensor_tensor(
                            out=ep[:, m, lo - base : hi - base], in0=sn[:, 0 : hi - lo],
                            scalar=amp[:, m : m + 1], in1=tbps[c][:, lo - base : hi - base],
                            op0=ALU.mult, op1=ALU.mult,
                        )
                        if c == 0 and lo == 0 and m == 3:
                            features()
                        if hi == CH[c][1] and m >= 4 - SE[c]:
                            empty_banks(1, True)
                        if c == WT_AT and m >= 1:
                            weight_copy(m - 1)
                        if c >= 1 and m == 1 and c + 1 < NCH:
                            broadcast_t(c + 1)
                empty_banks(VE[c], False)

            d = c - 1
            if d >= 0:
                wd = CH[d][1] - CH[d][0]
                eg = egpool.tile([P, 4 * CB], BF16, name="eg", align_bytes=64)
                gt = 0
                if c < NCH:
                    gt = GT if CH[c][1] - CH[c][0] == CB else GTS
                if gt:
                    nc.gpsimd.tensor_scalar(
                        out=eg[:, 0 : 4 * gt].rearrange("p (c k) -> p c k", k=4),
                        in0=eps[d][:, :, 0:gt].rearrange("p k c -> p c k"),
                        scalar1=1.0, scalar2=0.0, op0=ALU.mult, op1=ALU.add,
                    )
                regroup(eg[:, 4 * gt : 4 * wd], eps[d][:, :, gt:wd])
                quantise_pending()
                if d == WT_AT:
                    weight_quantise()
                for s in range(wd // GB):
                    half = slice(CH[d][0] + s * GB, CH[d][0] + (s + 1) * GB)
                    nc.vector.quantize_mx(
                        out=ec[:, half].bitcast(FP8X4), scales=es[:, half],
                        in_=eg[:, s * 4 * GB : (s + 1) * 4 * GB],
                    )
                    ready.add(CH[d][0] // GB + s)

        hps = {}

        ps1s = {}

        def layer1_matmuls(n):
            for i in range(state["mm1"], min(n, 4 * NG)):
                g, m = divmod(i, 4)
                if g not in ready:
                    return
                cols = slice(g * GB, (g + 1) * GB)
                ps1s[i] = new_bank([P, GB], F32)
                nc.tensor.matmul_mx(
                    out=ps1s[i][:],
                    lhsT=w1c[:, m * P : (m + 1) * P].bitcast(FP8X4),
                    lhsT_scale=w1s[:, m * P : (m + 1) * P],
                    rhs=ec[:, cols].bitcast(FP8X4),
                    rhs_scale=es[:, cols],
                    start=True, stop=True,
                )
                state["mm1"] = i + 1

        def layer1_tile(i, ahead):
            g, m = divmod(i, 4)
            layer1_matmuls(i + 1 + ahead)
            assert i < state["mm1"]
            if m == 0:
                hps[g] = ring.tile([P, 4, GB], BF16, name="hp", tag="ring", align_bytes=64)
            nc.scalar.activation(
                out=hps[g][:, m, :], in_=ps1s[i][:], func=ACT.Silu, bias=b1f[:, m : m + 1], scale=1.0
            )

        for i in range(PRE):
            layer1_tile(i, AH0)
            if i % LATE_EVERY == 1:
                if state["issued"] > state["next"] and state["next"] < NBE + NSL:
                    empty_banks(1, True)
                if state["issued"] < NBE + NSL + 1:
                    issue_to(state["issued"] + 1)

        out_v = out.rearrange("(g a p) o -> g p a o", a=4, p=P)
        hgs, hcs, hss, ps2s, zs = {}, {}, {}, {}, {}
        for k in range(NG + LSIL + 1):
            made = state["issued"]
            for i in range(PRE + RATE * k, min(PRE + RATE * (k + 1), 4 * NG)):
                layer1_tile(i, AH1)
            if k < NG:
                if k in hgs:
                    regroup(hgs[k][:, 4 * GH :], hps[k][:, :, GH:])
                else:
                    hgs[k] = hgpool.tile([P, 4 * GB], BF16, name="hg", align_bytes=64)
                    regroup(hgs[k][:], hps[k][:])
            g = k - 1
            if 0 <= g < NG:
                hcs[g] = cpool.tile([P, GB], U32, name="hc", align_bytes=64)
                hss[g] = cpool.tile([P, GB], U8, name="hs", align_bytes=64)
                nc.vector.quantize_mx(out=hcs[g][:].bitcast(FP8X4), scales=hss[g][:], in_=hgs[g][:])
                for s in range(2):
                    ps2 = new_bank([P, 2, O], F32)
                    ps2s[g, s] = ps2
                    for j in range(2):
                        bt = 2 * s + j
                        nc.tensor.matmul_mx(
                            out=ps2[:, j, :],
                            lhsT=hcs[g][:, bt * P : (bt + 1) * P].bitcast(FP8X4),
                            lhsT_scale=hss[g][:, bt * P : (bt + 1) * P],
                            rhs=w2c[:].bitcast(FP8X4),
                            rhs_scale=w2s[:],
                            start=True, stop=True,
                        )
            issue_to(state["issued"] + 1)
            ga = k - LADD
            if 0 <= ga < NG and k + 1 < NG:
                hgs[k + 1] = hgpool.tile([P, 4 * GB], BF16, name="hg", align_bytes=64)
                nc.gpsimd.tensor_scalar(
                    out=hgs[k + 1][:, 0 : 4 * GH].rearrange("p (c k) -> p c k", k=4),
                    in0=hps[k + 1][:, :, 0:GH].rearrange("p k c -> p c k"),
                    scalar1=1.0, scalar2=0.0, op0=ALU.mult, op1=ALU.add,
                )
            if 0 <= ga < NG:
                zs[ga] = zpool.tile([P, 4, O], F32, name="z")
                for s in range(2):
                    nc.vector.tensor_tensor(
                        out=zs[ga][:, 2 * s : 2 * s + 2, :], in0=ps2s[ga, s][:],
                        in1=b2f[:].unsqueeze(1).to_broadcast([P, 2, O]), op=ALU.add
                    )
            if state["next"] < made:
                empty_banks(1, False)
            quantise_pending()
            gs = k - LSIL
            if 0 <= gs < NG:
                parts = 2 if gs == NG - 1 else 1
                w = 4 // parts
                for s in range(parts):
                    zz = zs[gs][:, s * w : (s + 1) * w, :]
                    nc.scalar.activation(out=zz, in_=zz, func=ACT.Silu)
                    nc.sync.dma_start(out=out_v[gs][:, s * w : (s + 1) * w, :], in_=zz)
